import numpy as np
import ml_dtypes


def mxq(x, axis, fmt="e4m3"):
    dtype, down = {"e4m3": (ml_dtypes.float8_e4m3fn, 7), "e5m2": (ml_dtypes.float8_e5m2, 14)}[fmt]
    v = np.moveaxis(np.asarray(x, np.float32).astype(ml_dtypes.bfloat16).astype(np.float64), axis, -1)
    blocks = v.reshape(v.shape[:-1] + (-1, 32))
    amax = np.abs(blocks).max(-1, keepdims=True)
    byte = np.maximum(np.where(amax > 0, np.frexp(amax)[1] - 1 + 127, 0) - down, 1)
    scale = np.exp2(byte - 127.0)
    codes = (blocks / scale).astype(np.float32).astype(dtype).astype(np.float64)
    return np.moveaxis((codes * scale).reshape(v.shape), -1, axis)


WIDE = False


def mx_kscale(k):
    if not WIDE:
        return np.ones(k)
    levels = np.array([10, -10, 5, -5, 0])
    if k % 512:
        return np.exp2(np.random.permutation(np.resize(levels, k // 32))).repeat(32)
    a = np.empty((k // 512, 16))
    for p in range(k // 512):
        a[p, :8] = np.random.permutation(np.resize(levels, 8))
        for g in range(8):
            far = levels[np.abs(levels - a[p, g]) >= 10]
            a[p, g + 8] = far[np.random.randint(len(far))]
    return np.exp2(a.ravel()).repeat(32)


BF16 = ml_dtypes.bfloat16


def bf(x):
    return np.asarray(x, np.float32).astype(BF16)


def f64(x):
    return np.asarray(x).astype(np.float64)


B, T, C, CO, HS, DW, DA, DV, DG = 8, 1024, 1024, 256, 64, 128, 128, 128, 256


def sigmoid(u):
    return 1.0 / (1.0 + np.exp(-u))


def setup_inputs():
    n = np.random.standard_normal
    s = mx_kscale(C)
    return {
        "x": bf(n((B, T, C)) * s),
        "x_v": bf(n((1, 1, C)) * 0.3),
        "W_v": bf(n((CO, C)) / np.sqrt(C) / s),
        "v_hid": bf(n((B, T, DV))),
        "v2": bf(n((DV, CO)) / np.sqrt(DV)),
        "v0": bf(0.73 + n((1, 1, CO)) * 0.2),
        "v_first": bf(n((B, T, CO))),
    }


def reference(x, x_v, W_v, v_hid, v2, v0, v_first):
    x = f64(x)
    prev = np.concatenate([np.zeros_like(x[:, :1]), x[:, :-1]], axis=1)
    xv = x + (prev - x) * f64(x_v)
    v = mxq(xv, 2, "e4m3") @ mxq(f64(W_v), 1, "e4m3").T
    mix = sigmoid(f64(v0) + f64(v_hid) @ f64(v2))
    return v + (f64(v_first) - v) * mix

@@ -1,0 +1,344 @@
+from contextlib import ExitStack
+
+import concourse.mybir as mybir
+from concourse.masks import make_identity
+
+FP8X4 = mybir.dt.float8_e4m3fn_x4
+BF16 = mybir.dt.bfloat16
+F32 = mybir.dt.float32
+U32 = mybir.dt.uint32
+U8 = mybir.dt.uint8
+ALU = mybir.AluOpType
+ACT = mybir.ActivationFunctionType
+
+P = 128
+B, T, C, CO, DV = 8, 1024, 1024, 256, 128
+FLOPS = 2 * B * T * C * CO + 2 * B * T * DV * CO
+
+N_STEPS = 4 * B
+NG1 = 64
+X_AHEAD = 6
+LOAD_ORDER = (3, 0, 1, 2)
+
+
+def tile_full_tmix_params_pb_t_kernel(tc, x, x_v, W_v, v_hid, v2, v0, v_first, out):
+    nc = tc.nc
+    with ExitStack() as ctx:
+        const = ctx.enter_context(tc.tile_pool(name="const", bufs=1))
+        xin = ctx.enter_context(tc.tile_pool(name="xin", bufs=1))
+        seqp = ctx.enter_context(tc.tile_pool(name="seqp", bufs=3))
+        work = ctx.enter_context(tc.tile_pool(name="work", bufs=3))
+        ep = ctx.enter_context(tc.tile_pool(name="ep", bufs=3))
+        psum = ctx.enter_context(tc.psum_pool(name="psum", bufs=1))
+        ctx.enter_context(tc.manual_schedule())
+
+        x_tiles = {}
+
+        def load_x(k):
+            b, s = k // 4, LOAD_ORDER[k % 4]
+            if s == 3:
+                x_sb = xin.tile([P, 2, C], BF16, tag="x3", bufs=3, name="x3_sb")
+            else:
+                x_sb = xin.tile([P, 2, C], BF16, tag="x", bufs=6, name="x_sb")
+            src = x[b].rearrange("(p i s) c -> p i s c", i=2, s=4)
+            nc.sync.dma_start(out=x_sb[:], in_=src[:, :, s, :])
+            x_tiles[(b, s)] = x_sb
+
+        seq_tiles = {}
+
+        def load_seq(b):
+            vh = seqp.tile([P, 8, DV], BF16, name="vh")
+            nc.sync.dma_start(out=vh[:], in_=v_hid[b].rearrange("(p j) d -> p j d", j=8))
+            vf = seqp.tile([P, 8, CO], BF16, name="vf")
+            nc.sync.dma_start(out=vf[:], in_=v_first[b].rearrange("(p j) c -> p j c", j=8))
+            seq_tiles[b] = (vh, vf)
+
+        banks = {}
+        a_tiles = {}
+
+        def bank_tile(g):
+            if g == 0:
+                return psum.tile([P, 2, 2, P], F32, tag="xt0", bufs=2, name="xt0_ps")
+            return psum.tile([P, 2, 2, P], F32, tag="xt1", bufs=2, name="xt1_ps")
+
+        def as_planes(bk):
+            return bk[:].bitcast(BF16).rearrange("p u i (r e) -> p u i r e", e=2)
+
+        def transpose_x(b, s, g):
+            xw = x_tiles[(b, s)][:].bitcast(F32)
+            bk = bank_tile(g)
+            for u in range(2):
+                for i in range(2):
+                    nc.tensor.transpose(bk[:, u, i, :], xw[:, i, g * 2 * P + u : (g + 1) * 2 * P : 2], ident_f[:])
+            banks[(b, s, g)] = as_planes(bk)
+
+        def transpose_wrap(b, g):
+            xw = x_tiles[(b, 3)][:].bitcast(F32)
+            bk = bank_tile(g)
+            for u in range(2):
+                words = slice(g * 2 * P + u, (g + 1) * 2 * P, 2)
+                row = bk[:, u, :, :].rearrange("p i r -> p (i r)")
+                nc.tensor.transpose(row[:, 0:P], zeros_f[:], ident_f[:])
+                nc.tensor.transpose(row[:, 1 : P + 1], xw[:, 1, words], ident_f[:])
+                nc.tensor.transpose(row[:, P : 2 * P], xw[:, 0, words], ident_f[:])
+            banks[(b, -1, g)] = as_planes(bk)
+
+        def scale_x(n, g):
+            key = (n // 4, n % 4)
+            if g == 0:
+                a_tiles[key] = work.tile([P, 8, 2, P], F32, name="a")
+            a = a_tiles[key]
+            bv = banks[(key[0], key[1], g)]
+            for u in range(2):
+                for e in range(2):
+                    pl = 4 * g + 2 * u + e
+                    nc.scalar.activation(
+                        out=a[:, pl, :, :], in_=bv[:, u, :, :, e], func=ACT.Copy,
+                        scale=om[:, pl : pl + 1],
+                    )
+
+        xvp_tiles = {}
+
+        def mix(n, g):
+            b, s = n // 4, n % 4
+            prev = banks[(b, s - 1, g)]
+            a = a_tiles[(b, s)]
+            if g == 0:
+                xvp_tiles[n] = work.tile([P, 8, 2, P], BF16, name="xvp")
+            xvp = xvp_tiles[n]
+            for u in range(2):
+                for e in range(2):
+                    pl = 4 * g + 2 * u + e
+                    nc.vector.scalar_tensor_tensor(
+                        out=xvp[:, pl, :, :], in0=prev[:, u, :, :, e], scalar=m[:, pl : pl + 1],
+                        in1=a[:, pl, :, :], op0=ALU.mult, op1=ALU.add,
+                    )
+
+        grp_tiles = {}
+
+        def regroup_pool(n, g, lo, hi):
+            if g == 0:
+                grp_tiles[n] = work.tile([P, 2, 2 * P, 4], BF16, tag="grp", bufs=1, name="grp", align_bytes=64)
+            src = xvp_tiles[n][:].rearrange("p (g t) i r -> p g (i r) t", g=2)
+            nc.gpsimd.tensor_scalar(
+                out=grp_tiles[n][:, g, lo:hi, :], in0=src[:, g, lo:hi, :], scalar1=1.0, scalar2=0.0,
+                op0=ALU.mult, op1=ALU.add,
+            )
+
+        def regroup_act(n, g, lo, hi):
+            src = xvp_tiles[n][:].rearrange("p (g t) i r -> p g t (i r)", g=2)
+            nc.scalar.copy(
+                out=grp_tiles[n][:, g, lo:hi, :].rearrange("p (c i) t -> p c t i", i=4),
+                in_=src[:, g, :, lo:hi].rearrange("p t (c i) -> p c t i", i=4),
+            )
+
+        g_tiles = {}
+
+        def gate(n):
+            b, s = n // 4, n % 4
+            vht = vht_tiles[b]
+            g_ps = psum.tile([P, 2, CO], F32, tag="g", bufs=1, name="g_ps")
+            for i in range(2):
+                for h in range(2):
+                    nc.tensor.matmul(
+                        out=g_ps[:, i, h * P : (h + 1) * P], lhsT=v0_wide[:, h, :], rhs=ident_f[:],
+                        is_transpose=True, start=(h == 0), stop=False,
+                    )
+                nc.tensor.matmul(
+                    out=g_ps[:, i, :], lhsT=vht[:, 4 * i + s, :], rhs=v2_sb[:], start=False, stop=True
+                )
+            g_tiles[n] = g_ps
+
+        mix_tiles = {}
+
+        def sigmoid(n):
+            mx_t = ep.tile([P, 2, CO], F32, name="mix_sb")
+            nc.scalar.activation(out=mx_t[:], in_=g_tiles[n][:], func=ACT.Sigmoid)
+            mix_tiles[n] = mx_t
+
+        q_tiles = {}
+
+        def quantise(n):
+            xc = work.tile([P, 4 * P], U32, name="xc", align_bytes=64)
+            xs = work.tile([P, 4 * P], U8, name="xs", align_bytes=64)
+            nc.vector.quantize_mx(
+                out=xc[:].bitcast(FP8X4), scales=xs[:],
+                in_=grp_tiles[n][:].rearrange("p g n t -> p (g n t)"),
+            )
+            q_tiles[n] = (xc, xs)
+
+        v_tiles = {}
+
+        def project(n):
+            xc, xs = q_tiles[n]
+            v_ps = psum.tile([P, 2, CO], F32, tag="v", bufs=2, name="v_ps")
+            for i in range(2):
+                for g in range(2):
+                    c0 = g * 2 * P + i * P
+                    nc.tensor.matmul_mx(
+                        out=v_ps[:, i, :],
+                        lhsT=xc[:, c0 : c0 + P].bitcast(FP8X4),
+                        lhsT_scale=xs[:, c0 : c0 + P],
+                        rhs=w_codes[:, g * CO : (g + 1) * CO].bitcast(FP8X4),
+                        rhs_scale=w_scales[:, g * CO : (g + 1) * CO],
+                        start=(g == 0),
+                        stop=(g == 1),
+                    )
+            v_tiles[n] = v_ps
+
+        e_tiles = {}
+        f_tiles = {}
+
+        def blend_sub(n):
+            b, s = n // 4, n % 4
+            vf = seq_tiles[b][1][:].rearrange("p (i s) c -> p i s c", s=4)[:, :, s, :]
+            e_sb = ep.tile([P, 2, CO], F32, name="e_sb")
+            nc.vector.tensor_tensor(out=e_sb[:], in0=vf, in1=v_tiles[n][:], op=ALU.subtract)
+            e_tiles[n] = e_sb
+
+        def blend_mul(n):
+            f_sb = ep.tile([P, 2, CO], F32, name="f_sb")
+            if n < N_STEPS - 2:
+                nc.gpsimd.tensor_tensor(out=f_sb[:], in0=e_tiles[n][:], in1=mix_tiles[n][:], op=ALU.mult)
+            else:
+                nc.vector.tensor_tensor(out=f_sb[:], in0=e_tiles[n][:], in1=mix_tiles[n][:], op=ALU.mult)
+            f_tiles[n] = f_sb
+
+        def blend_add(n):
+            b, s = n // 4, n % 4
+            o_sb = ep.tile([P, 2, CO], F32, name="o_sb")
+            nc.vector.tensor_tensor(out=o_sb[:], in0=f_tiles[n][:], in1=v_tiles[n][:], op=ALU.add)
+            dst = out[b].rearrange("(p i s) c -> p i s c", i=2, s=4)
+            nc.sync.dma_start(out=dst[:, :, s, :], in_=o_sb[:])
+
+        vht_tiles = {}
+        vh_banks = {}
+
+        def transpose_vh(b):
+            vh = seq_tiles[b][0]
+            vh_ps = psum.tile([P, 8, P], BF16, tag="st", bufs=1, name="vh_ps")
+            for j in range(8):
+                nc.tensor.transpose(vh_ps[:, j, :], vh[:, j, :], ident_b[:])
+            vh_banks[b] = vh_ps
+
+        def copy_vh(b):
+            vht = seqp.tile([P, 8, P], BF16, name="vht")
+            nc.scalar.copy(out=vht[:], in_=vh_banks[b][:])
+            vht_tiles[b] = vht
+
+        xv_rows = const.tile([P, 2 * P], F32, name="xv_rows")
+        nc.vector.memset(xv_rows[:], 0.0)
+        nc.sync.dma_start(
+            out=xv_rows[:].bitcast(BF16)[0:2, :],
+            in_=x_v.rearrange("a b (r c) -> (a b r) c", r=2),
+        )
+        load_x(0)
+        load_x(1)
+        w_sb = const.tile([P, 2, C], BF16, name="w_sb")
+        nc.sync.dma_start(out=w_sb[:], in_=W_v.rearrange("(h p) c -> p h c", p=P))
+        v0_rows = const.tile([P, P], BF16, name="v0_rows")
+        nc.vector.memset(v0_rows[:], 0.0)
+        nc.sync.dma_start(out=v0_rows[0:2, :], in_=v0.rearrange("a b (h c) -> (a b h) c", h=2))
+        v2_sb = const.tile([P, CO], BF16, name="v2_sb")
+        nc.sync.dma_start(out=v2_sb[:], in_=v2)
+        load_seq(0)
+        for k in range(2, X_AHEAD):
+            load_x(k)
+        load_seq(1)
+
+        ident_f = const.tile([P, P], F32, name="ident_f")
+        make_identity(nc, ident_f[:])
+        ident_b = const.tile([P, P], BF16, name="ident_b")
+        make_identity(nc, ident_b[:])
+        zeros_f = const.tile([P, P], F32, name="zeros_f")
+        nc.vector.memset(zeros_f[:], 0.0)
+
+        xv_ps = psum.tile([P, 2, P], F32, tag="st", bufs=1, name="xv_ps")
+        for u in range(2):
+            nc.tensor.transpose(xv_ps[:, u, :], xv_rows[:, u : 2 * P : 2], ident_f[:])
+        m = const.tile([P, 8], F32, name="m")
+        xv_planes = xv_ps[:].bitcast(BF16).rearrange("p u (g e) -> p u g e", e=2)[:, :, 0:2, :]
+        nc.vector.tensor_copy(out=m[:].rearrange("p (g u e) -> p u g e", g=2, u=2), in_=xv_planes)
+        om = const.tile([P, 8], F32, name="om")
+        nc.vector.tensor_scalar(
+            out=om[:], in0=m[:], scalar1=-1.0, scalar2=1.0, op0=ALU.mult, op1=ALU.add
+        )
+        transpose_wrap(0, 0)
+        transpose_x(0, 0, 0)
+        scale_x(0, 0)
+        transpose_wrap(0, 1)
+        transpose_x(0, 0, 1)
+
+        v0_ps = psum.tile([P, P], BF16, tag="st", bufs=1, name="v0_ps")
+        nc.tensor.transpose(v0_ps[:], v0_rows[:], ident_b[:])
+        v0_col = const.tile([P, 2], F32, name="v0_col")
+        nc.vector.tensor_copy(out=v0_col[:], in_=v0_ps[:, 0:2])
+        v0_wide = const.tile([P, 2, P], F32, name="v0_wide")
+        nc.vector.tensor_copy(out=v0_wide[:], in_=v0_col[:].unsqueeze(2).to_broadcast([P, 2, P]))
+
+        w_words = w_sb[:].bitcast(F32)
+        w_grp = const.tile([P, 2, CO, 4], BF16, name="w_grp", align_bytes=64)
+        w_grp_words = w_grp[:].bitcast(F32)
+        for g in range(2):
+            w_ps = psum.tile([P, 2, 2, P], F32, tag="v", bufs=2, name="w_ps")
+            for u in range(2):
+                for h in range(2):
+                    nc.tensor.transpose(w_ps[:, u, h, :], w_words[:, h, g * 2 * P + u : (g + 1) * 2 * P : 2], ident_f[:])
+            nc.vector.tensor_copy(
+                out=w_grp_words[:, g, :, :], in_=w_ps[:].rearrange("p u h r -> p (h r) u")
+            )
+        w_codes = const.tile([P, 2 * CO], U32, name="w_codes", align_bytes=64)
+        w_scales = const.tile([P, 2 * CO], U8, name="w_scales", align_bytes=64)
+        nc.vector.quantize_mx(
+            out=w_codes[:].bitcast(FP8X4), scales=w_scales[:],
+            in_=w_grp[:].rearrange("p g c t -> p (g c t)"),
+        )
+        transpose_vh(0)
+        copy_vh(0)
+
+        def live(n):
+            return 0 <= n < N_STEPS
+
+        def refill(n, g):
+            b, s = n // 4, n % 4
+            if s < 3:
+                transpose_x(b, s + 1, g)
+            elif b + 1 < B:
+                transpose_x(b + 1, 0, g)
+                transpose_wrap(b + 1, g)
+
+        for n in range(N_STEPS + 3):
+            if n + X_AHEAD < N_STEPS:
+                load_x(n + X_AHEAD)
+            if n % 4 == 2 and n // 4 + 2 < B:
+                load_seq(n // 4 + 2)
+            if live(n):
+                mix(n, 0)
+            if live(n - 1):
+                regroup_act(n - 1, 1, NG1, 2 * P)
+                sigmoid(n - 1)
+            if live(n):
+                refill(n, 0)
+                gate(n)
+            if n % 4 == 1 and n // 4 + 1 < B:
+                transpose_vh(n // 4 + 1)
+            if live(n):
+                scale_x(n, 1)
+            if live(n - 3):
+                blend_add(n - 3)
+            if live(n - 1):
+                quantise(n - 1)
+                project(n - 1)
+            if live(n):
+                regroup_pool(n, 0, 0, 2 * P)
+            if live(n - 2):
+                blend_sub(n - 2)
+                blend_mul(n - 2)
+            if live(n + 1):
+                scale_x(n + 1, 0)
+            if n % 4 == 1 and n // 4 + 1 < B:
+                copy_vh(n // 4 + 1)
+            if live(n):
+                mix(n, 1)
+                refill(n, 1)
+                regroup_pool(n, 1, 0, NG1)

@@ -15,34 +15,39 @@ P = 128
 B, T, C, CO, DV = 8, 1024, 1024, 256, 128
 FLOPS = 2 * B * T * C * CO + 2 * B * T * DV * CO
 
-N_STEPS = 4 * B
-NG1 = 64
-X_AHEAD = 6
-LOAD_ORDER = (3, 0, 1, 2)
+H = 512
+NT = H // P
+N_STEPS = B * T // H
+X_BUFS = 5
+R_POOL = 256
+R_ACT = 192
+FORM = (1, 2)
+L_POOL = 128
+L_ACT = 192
 
 
 def tile_full_tmix_params_pb_t_kernel(tc, x, x_v, W_v, v_hid, v2, v0, v_first, out):
     nc = tc.nc
     with ExitStack() as ctx:
         const = ctx.enter_context(tc.tile_pool(name="const", bufs=1))
-        xin = ctx.enter_context(tc.tile_pool(name="xin", bufs=1))
+        xin = ctx.enter_context(tc.tile_pool(name="xin", bufs=X_BUFS))
         seqp = ctx.enter_context(tc.tile_pool(name="seqp", bufs=3))
-        work = ctx.enter_context(tc.tile_pool(name="work", bufs=3))
+        work = ctx.enter_context(tc.tile_pool(name="work", bufs=2))
         ep = ctx.enter_context(tc.tile_pool(name="ep", bufs=3))
         psum = ctx.enter_context(tc.psum_pool(name="psum", bufs=1))
         ctx.enter_context(tc.manual_schedule())
 
         x_tiles = {}
 
-        def load_x(k):
-            b, s = k // 4, LOAD_ORDER[k % 4]
-            if s == 3:
-                x_sb = xin.tile([P, 2, C], BF16, tag="x3", bufs=3, name="x3_sb")
+        def load_x(n):
+            x_sb = xin.tile([P, NT, C], BF16, name="x_sb")
+            src = x[n // 2].rearrange("(h i p) c -> h p i c", h=2, p=P)
+            if n == 0:
+                for c0 in (0, C // 2):
+                    nc.sync.dma_start(out=x_sb[:, :, c0 : c0 + C // 2], in_=src[0, :, :, c0 : c0 + C // 2])
             else:
-                x_sb = xin.tile([P, 2, C], BF16, tag="x", bufs=6, name="x_sb")
-            src = x[b].rearrange("(p i s) c -> p i s c", i=2, s=4)
-            nc.sync.dma_start(out=x_sb[:], in_=src[:, :, s, :])
-            x_tiles[(b, s)] = x_sb
+                nc.sync.dma_start(out=x_sb[:], in_=src[n % 2])
+            x_tiles[n] = x_sb
 
         seq_tiles = {}
 
@@ -50,190 +55,199 @@ def tile_full_tmix_params_pb_t_kernel(tc, x, x_v, W_v, v_hid, v2, v0, v_first, o
             vh = seqp.tile([P, 8, DV], BF16, name="vh")
             nc.sync.dma_start(out=vh[:], in_=v_hid[b].rearrange("(p j) d -> p j d", j=8))
             vf = seqp.tile([P, 8, CO], BF16, name="vf")
-            nc.sync.dma_start(out=vf[:], in_=v_first[b].rearrange("(p j) c -> p j c", j=8))
+            nc.sync.dma_start(out=vf[:], in_=v_first[b].rearrange("(i p) c -> p i c", p=P))
             seq_tiles[b] = (vh, vf)
 
         banks = {}
-        a_tiles = {}
 
-        def bank_tile(g):
-            if g == 0:
-                return psum.tile([P, 2, 2, P], F32, tag="xt0", bufs=2, name="xt0_ps")
-            return psum.tile([P, 2, 2, P], F32, tag="xt1", bufs=2, name="xt1_ps")
+        def transpose_x(n, k):
+            g, u = k // 2, k % 2
+            xw = x_tiles[n][:].bitcast(F32)
+            bk = psum.tile([P, NT, P], F32, tag="xt", bufs=4, name="xt_ps")
+            for i in range(NT):
+                nc.tensor.transpose(bk[:, i, :], xw[:, i, g * 2 * P + u : (g + 1) * 2 * P : 2], ident_f[:])
+            banks[(n, k)] = bk[:].bitcast(BF16).rearrange("p i (r e) -> p (i r) e", e=2)
 
-        def as_planes(bk):
-            return bk[:].bitcast(BF16).rearrange("p u i (r e) -> p u i r e", e=2)
-
-        def transpose_x(b, s, g):
-            xw = x_tiles[(b, s)][:].bitcast(F32)
-            bk = bank_tile(g)
-            for u in range(2):
-                for i in range(2):
-                    nc.tensor.transpose(bk[:, u, i, :], xw[:, i, g * 2 * P + u : (g + 1) * 2 * P : 2], ident_f[:])
-            banks[(b, s, g)] = as_planes(bk)
-
-        def transpose_wrap(b, g):
-            xw = x_tiles[(b, 3)][:].bitcast(F32)
-            bk = bank_tile(g)
-            for u in range(2):
-                words = slice(g * 2 * P + u, (g + 1) * 2 * P, 2)
-                row = bk[:, u, :, :].rearrange("p i r -> p (i r)")
-                nc.tensor.transpose(row[:, 0:P], zeros_f[:], ident_f[:])
-                nc.tensor.transpose(row[:, 1 : P + 1], xw[:, 1, words], ident_f[:])
-                nc.tensor.transpose(row[:, P : 2 * P], xw[:, 0, words], ident_f[:])
-            banks[(b, -1, g)] = as_planes(bk)
-
-        def scale_x(n, g):
-            key = (n // 4, n % 4)
-            if g == 0:
-                a_tiles[key] = work.tile([P, 8, 2, P], F32, name="a")
-            a = a_tiles[key]
-            bv = banks[(key[0], key[1], g)]
-            for u in range(2):
-                for e in range(2):
-                    pl = 4 * g + 2 * u + e
-                    nc.scalar.activation(
-                        out=a[:, pl, :, :], in_=bv[:, u, :, :, e], func=ACT.Copy,
-                        scale=om[:, pl : pl + 1],
-                    )
+        def scale_x(n, k):
+            a = a_tiles[(n // 2) % 2]
+            c0 = 1 + (n % 2) * H
+            for e in range(2):
+                pl = 2 * k + e
+                nc.scalar.activation(
+                    out=a[:, pl, c0 : c0 + H], in_=banks[(n, k)][:, :, e], func=ACT.Copy, scale=m[:, pl : pl + 1]
+                )
 
         xvp_tiles = {}
 
-        def mix(n, g):
-            b, s = n // 4, n % 4
-            prev = banks[(b, s - 1, g)]
-            a = a_tiles[(b, s)]
-            if g == 0:
-                xvp_tiles[n] = work.tile([P, 8, 2, P], BF16, name="xvp")
-            xvp = xvp_tiles[n]
-            for u in range(2):
-                for e in range(2):
-                    pl = 4 * g + 2 * u + e
-                    nc.vector.scalar_tensor_tensor(
-                        out=xvp[:, pl, :, :], in0=prev[:, u, :, :, e], scalar=m[:, pl : pl + 1],
-                        in1=a[:, pl, :, :], op0=ALU.mult, op1=ALU.add,
-                    )
+        def mix(n, k):
+            a = a_tiles[(n // 2) % 2]
+            c0 = (n % 2) * H
+            if k == 0:
+                xvp_tiles[n] = work.tile([P, 8, H], BF16, name="xvp", bufs=3)
+            for e in range(2):
+                pl = 2 * k + e
+                nc.vector.scalar_tensor_tensor(
+                    out=xvp_tiles[n][:, pl, :], in0=banks[(n, k)][:, :, e], scalar=om[:, pl : pl + 1],
+                    in1=a[:, pl, c0 : c0 + H], op0=ALU.mult, op1=ALU.add,
+                )
 
         grp_tiles = {}
 
-        def regroup_pool(n, g, lo, hi):
-            if g == 0:
-                grp_tiles[n] = work.tile([P, 2, 2 * P, 4], BF16, tag="grp", bufs=1, name="grp", align_bytes=64)
-            src = xvp_tiles[n][:].rearrange("p (g t) i r -> p g (i r) t", g=2)
+        def grp(n):
+            if n not in grp_tiles:
+                grp_tiles[n] = work.tile([P, 2, H, 4], BF16, name="grp", bufs=1, align_bytes=64)
+            return grp_tiles[n]
+
+        def quad_views(n, g, lo, hi):
+            dst = grp(n)[:, g, lo:hi, :].rearrange("p (c i) t -> p c t i", i=4)
+            src = xvp_tiles[n][:, 4 * g : 4 * g + 4, lo:hi].rearrange("p t (c i) -> p c t i", i=4)
+            return dst, src
+
+        def regroup_pool(n, g, hi=R_POOL):
+            src = xvp_tiles[n][:, 4 * g : 4 * g + 4, 0:hi].rearrange("p t n -> p n t")
             nc.gpsimd.tensor_scalar(
-                out=grp_tiles[n][:, g, lo:hi, :], in0=src[:, g, lo:hi, :], scalar1=1.0, scalar2=0.0,
-                op0=ALU.mult, op1=ALU.add,
+                out=grp(n)[:, g, 0:hi, :], in0=src, scalar1=1.0, scalar2=0.0, op0=ALU.mult, op1=ALU.add
             )
 
-        def regroup_act(n, g, lo, hi):
-            src = xvp_tiles[n][:].rearrange("p (g t) i r -> p g t (i r)", g=2)
-            nc.scalar.copy(
-                out=grp_tiles[n][:, g, lo:hi, :].rearrange("p (c i) t -> p c t i", i=4),
-                in_=src[:, g, :, lo:hi].rearrange("p t (c i) -> p c t i", i=4),
+        def regroup_act(n, g, lo=R_POOL, hi=R_POOL + R_ACT):
+            dst, src = quad_views(n, g, lo, hi)
+            nc.scalar.copy(out=dst, in_=src)
+
+        def regroup_vec(n, g, lo=R_POOL + R_ACT):
+            dst, src = quad_views(n, g, lo, H)
+            nc.vector.tensor_copy(out=dst, in_=src)
+
+        q_tiles = {}
+
+        def quantise(n, halves=(0, 2)):
+            lo, hi = halves
+            if lo == 0:
+                xc = work.tile([P, 2 * H], U32, name="xc", align_bytes=64)
+                xs = work.tile([P, 2 * H], U8, name="xs", align_bytes=64)
+                q_tiles[n] = (xc, xs)
+            xc, xs = q_tiles[n]
+            nc.vector.quantize_mx(
+                out=xc[:, lo * H : hi * H].bitcast(FP8X4), scales=xs[:, lo * H : hi * H],
+                in_=grp(n)[:, lo:hi].rearrange("p g n t -> p (g n t)"),
             )
+
+        v_tiles = {}
+
+        def project(n):
+            xc, xs = q_tiles[n]
+            for j in range(2):
+                v_ps = psum.tile([P, 2, CO], F32, tag="v", bufs=2, name="v_ps")
+                for i in range(2):
+                    for g in range(2):
+                        c0 = g * H + (2 * j + i) * P
+                        nc.tensor.matmul_mx(
+                            out=v_ps[:, i, :],
+                            lhsT=xc[:, c0 : c0 + P].bitcast(FP8X4),
+                            lhsT_scale=xs[:, c0 : c0 + P],
+                            rhs=w_codes[:, g * CO : (g + 1) * CO].bitcast(FP8X4),
+                            rhs_scale=w_scales[:, g * CO : (g + 1) * CO],
+                            start=(g == 0),
+                            stop=(g == 1),
+                        )
+                v_tiles[(n, j)] = v_ps
 
         g_tiles = {}
 
-        def gate(n):
-            b, s = n // 4, n % 4
-            vht = vht_tiles[b]
-            g_ps = psum.tile([P, 2, CO], F32, tag="g", bufs=1, name="g_ps")
+        def gate(n, j):
+            vht = vht_tiles[n // 2]
+            g_ps = psum.tile([P, 2, CO], F32, tag="g", bufs=2, name="g_ps")
             for i in range(2):
                 for h in range(2):
                     nc.tensor.matmul(
                         out=g_ps[:, i, h * P : (h + 1) * P], lhsT=v0_wide[:, h, :], rhs=ident_f[:],
                         is_transpose=True, start=(h == 0), stop=False,
                     )
-                nc.tensor.matmul(
-                    out=g_ps[:, i, :], lhsT=vht[:, 4 * i + s, :], rhs=v2_sb[:], start=False, stop=True
-                )
-            g_tiles[n] = g_ps
+                t0 = (n % 2) * H + (2 * j + i) * P
+                nc.tensor.matmul(out=g_ps[:, i, :], lhsT=vht[:, t0 : t0 + P], rhs=v2_sb[:], start=False, stop=True)
+            g_tiles[(n, j)] = g_ps
 
         mix_tiles = {}
 
-        def sigmoid(n):
-            mx_t = ep.tile([P, 2, CO], F32, name="mix_sb")
-            nc.scalar.activation(out=mx_t[:], in_=g_tiles[n][:], func=ACT.Sigmoid)
-            mix_tiles[n] = mx_t
-
-        q_tiles = {}
-
-        def quantise(n):
-            xc = work.tile([P, 4 * P], U32, name="xc", align_bytes=64)
-            xs = work.tile([P, 4 * P], U8, name="xs", align_bytes=64)
-            nc.vector.quantize_mx(
-                out=xc[:].bitcast(FP8X4), scales=xs[:],
-                in_=grp_tiles[n][:].rearrange("p g n t -> p (g n t)"),
-            )
-            q_tiles[n] = (xc, xs)
-
-        v_tiles = {}
-
-        def project(n):
-            xc, xs = q_tiles[n]
-            v_ps = psum.tile([P, 2, CO], F32, tag="v", bufs=2, name="v_ps")
-            for i in range(2):
-                for g in range(2):
-                    c0 = g * 2 * P + i * P
-                    nc.tensor.matmul_mx(
-                        out=v_ps[:, i, :],
-                        lhsT=xc[:, c0 : c0 + P].bitcast(FP8X4),
-                        lhsT_scale=xs[:, c0 : c0 + P],
-                        rhs=w_codes[:, g * CO : (g + 1) * CO].bitcast(FP8X4),
-                        rhs_scale=w_scales[:, g * CO : (g + 1) * CO],
-                        start=(g == 0),
-                        stop=(g == 1),
-                    )
-            v_tiles[n] = v_ps
+        def sigmoid(n, j):
+            mx_t = ep.tile([P, 2, CO], F32, name="mix_sb", tag="mix%d" % j)
+            nc.scalar.activation(out=mx_t[:], in_=g_tiles[(n, j)][:], func=ACT.Sigmoid)
+            mix_tiles[(n, j)] = mx_t
 
         e_tiles = {}
         f_tiles = {}
+        o_tiles = {}
 
-        def blend_sub(n):
-            b, s = n // 4, n % 4
-            vf = seq_tiles[b][1][:].rearrange("p (i s) c -> p i s c", s=4)[:, :, s, :]
-            e_sb = ep.tile([P, 2, CO], F32, name="e_sb")
-            nc.vector.tensor_tensor(out=e_sb[:], in0=vf, in1=v_tiles[n][:], op=ALU.subtract)
-            e_tiles[n] = e_sb
+        def out_half(n, j):
+            if n not in o_tiles:
+                o_tiles[n] = ep.tile([P, NT, CO], F32, name="o_sb")
+            return o_tiles[n][:, 2 * j : 2 * j + 2, :]
 
-        def blend_mul(n):
-            f_sb = ep.tile([P, 2, CO], F32, name="f_sb")
-            if n < N_STEPS - 2:
-                nc.gpsimd.tensor_tensor(out=f_sb[:], in0=e_tiles[n][:], in1=mix_tiles[n][:], op=ALU.mult)
-            else:
-                nc.vector.tensor_tensor(out=f_sb[:], in0=e_tiles[n][:], in1=mix_tiles[n][:], op=ALU.mult)
-            f_tiles[n] = f_sb
+        def v_first_half(n, j):
+            i0 = (n % 2) * NT + 2 * j
+            return seq_tiles[n // 2][1][:, i0 : i0 + 2, :]
 
-        def blend_add(n):
-            b, s = n // 4, n % 4
-            o_sb = ep.tile([P, 2, CO], F32, name="o_sb")
-            nc.vector.tensor_tensor(out=o_sb[:], in0=f_tiles[n][:], in1=v_tiles[n][:], op=ALU.add)
-            dst = out[b].rearrange("(p i s) c -> p i s c", i=2, s=4)
-            nc.sync.dma_start(out=dst[:, :, s, :], in_=o_sb[:])
+        def sub_1(n, j):
+            e_sb = ep.tile([P, 2, CO], F32, name="e_sb", tag="e%d" % j, bufs=2)
+            nc.vector.tensor_tensor(out=e_sb[:], in0=v_first_half(n, j), in1=v_tiles[(n, j)][:], op=ALU.subtract)
+            e_tiles[(n, j)] = e_sb
+
+        def mul_1(n, j):
+            f_sb = ep.tile([P, 2, CO], F32, name="f_sb", tag="f%d" % j, bufs=2)
+            nc.gpsimd.tensor_tensor(out=f_sb[:], in0=e_tiles[(n, j)][:], in1=mix_tiles[(n, j)][:], op=ALU.mult)
+            f_tiles[(n, j)] = f_sb
+
+        def add_1(n, j):
+            nc.vector.tensor_tensor(out=out_half(n, j), in0=f_tiles[(n, j)][:], in1=v_tiles[(n, j)][:], op=ALU.add)
+
+        def store_half(n, j):
+            dst = out[n // 2].rearrange("(h j i p) c -> h j p i c", h=2, j=2, p=P)
+            nc.sync.dma_start(out=dst[n % 2, j], in_=out_half(n, j))
+
+        def mul_2(n, j):
+            f_sb = ep.tile([P, 2, CO], F32, name="f_sb", tag="f%d" % j, bufs=2)
+            nc.gpsimd.tensor_tensor(out=f_sb[:], in0=mix_tiles[(n, j)][:], in1=v_first_half(n, j), op=ALU.mult)
+            f_tiles[(n, j)] = f_sb
+
+        def own_2(n, j):
+            e_sb = ep.tile([P, 2, CO], F32, name="e_sb", tag="e%d" % j, bufs=2)
+            nc.vector.scalar_tensor_tensor(
+                out=e_sb[:], in0=mix_tiles[(n, j)][:], scalar=1.0, in1=v_tiles[(n, j)][:],
+                op0=ALU.subtract, op1=ALU.mult,
+            )
+            e_tiles[(n, j)] = e_sb
+
+        def sub_2(n, j, eng=nc.gpsimd):
+            eng.tensor_tensor(
+                out=out_half(n, j), in0=f_tiles[(n, j)][:], in1=e_tiles[(n, j)][:], op=ALU.subtract
+            )
+
+        def store(n):
+            dst = out[n // 2].rearrange("(h i p) c -> h p i c", h=2, p=P)
+            nc.sync.dma_start(out=dst[n % 2], in_=o_tiles[n][:])
 
         vht_tiles = {}
         vh_banks = {}
 
         def transpose_vh(b):
             vh = seq_tiles[b][0]
-            vh_ps = psum.tile([P, 8, P], BF16, tag="st", bufs=1, name="vh_ps")
+            vh_ps = psum.tile([P, 8, P], BF16, tag="g", bufs=2, name="vh_ps")
             for j in range(8):
                 nc.tensor.transpose(vh_ps[:, j, :], vh[:, j, :], ident_b[:])
             vh_banks[b] = vh_ps
 
         def copy_vh(b):
-            vht = seqp.tile([P, 8, P], BF16, name="vht")
-            nc.scalar.copy(out=vht[:], in_=vh_banks[b][:])
+            vht = seqp.tile([P, T], BF16, name="vht")
+            nc.scalar.copy(
+                out=vht[:].rearrange("d (p j) -> d p j", j=8), in_=vh_banks[b][:].rearrange("d j p -> d p j")
+            )
             vht_tiles[b] = vht
 
         xv_rows = const.tile([P, 2 * P], F32, name="xv_rows")
         nc.vector.memset(xv_rows[:], 0.0)
         nc.sync.dma_start(
-            out=xv_rows[:].bitcast(BF16)[0:2, :],
-            in_=x_v.rearrange("a b (r c) -> (a b r) c", r=2),
+            out=xv_rows[:].bitcast(BF16)[0:2, :], in_=x_v.rearrange("a b (r c) -> (a b r) c", r=2)
         )
         load_x(0)
-        load_x(1)
         w_sb = const.tile([P, 2, C], BF16, name="w_sb")
         nc.sync.dma_start(out=w_sb[:], in_=W_v.rearrange("(h p) c -> p h c", p=P))
         v0_rows = const.tile([P, P], BF16, name="v0_rows")
@@ -242,18 +256,23 @@ def tile_full_tmix_params_pb_t_kernel(tc, x, x_v, W_v, v_hid, v2, v0, v_first, o
         v2_sb = const.tile([P, CO], BF16, name="v2_sb")
         nc.sync.dma_start(out=v2_sb[:], in_=v2)
         load_seq(0)
-        for k in range(2, X_AHEAD):
-            load_x(k)
+        load_x(1)
+        load_x(2)
         load_seq(1)
+        for n in range(3, X_BUFS):
+            load_x(n)
 
         ident_f = const.tile([P, P], F32, name="ident_f")
         make_identity(nc, ident_f[:])
         ident_b = const.tile([P, P], BF16, name="ident_b")
         make_identity(nc, ident_b[:])
-        zeros_f = const.tile([P, P], F32, name="zeros_f")
-        nc.vector.memset(zeros_f[:], 0.0)
+        a_tiles = []
+        for j in range(2):
+            a_sb = const.tile([P, 8, 1 + T], F32, name="a%d" % j)
+            nc.gpsimd.memset(a_sb[:, :, 0:1], 0.0)
+            a_tiles.append(a_sb)
 
-        xv_ps = psum.tile([P, 2, P], F32, tag="st", bufs=1, name="xv_ps")
+        xv_ps = psum.tile([P, 2, P], F32, tag="g", bufs=2, name="xv_ps")
         for u in range(2):
             nc.tensor.transpose(xv_ps[:, u, :], xv_rows[:, u : 2 * P : 2], ident_f[:])
         m = const.tile([P, 8], F32, name="m")
@@ -263,13 +282,13 @@ def tile_full_tmix_params_pb_t_kernel(tc, x, x_v, W_v, v_hid, v2, v0, v_first, o
         nc.vector.tensor_scalar(
             out=om[:], in0=m[:], scalar1=-1.0, scalar2=1.0, op0=ALU.mult, op1=ALU.add
         )
-        transpose_wrap(0, 0)
-        transpose_x(0, 0, 0)
-        scale_x(0, 0)
-        transpose_wrap(0, 1)
-        transpose_x(0, 0, 1)
+        for k in range(4):
+            transpose_x(0, k)
+        for k in range(4):
+            scale_x(0, k)
+        mix(0, 0)
 
-        v0_ps = psum.tile([P, P], BF16, tag="st", bufs=1, name="v0_ps")
+        v0_ps = psum.tile([P, P], BF16, tag="g", bufs=2, name="v0_ps")
         nc.tensor.transpose(v0_ps[:], v0_rows[:], ident_b[:])
         v0_col = const.tile([P, 2], F32, name="v0_col")
         nc.vector.tensor_copy(out=v0_col[:], in_=v0_ps[:, 0:2])
@@ -283,7 +302,9 @@ def tile_full_tmix_params_pb_t_kernel(tc, x, x_v, W_v, v_hid, v2, v0, v_first, o
             w_ps = psum.tile([P, 2, 2, P], F32, tag="v", bufs=2, name="w_ps")
             for u in range(2):
                 for h in range(2):
-                    nc.tensor.transpose(w_ps[:, u, h, :], w_words[:, h, g * 2 * P + u : (g + 1) * 2 * P : 2], ident_f[:])
+                    nc.tensor.transpose(
+                        w_ps[:, u, h, :], w_words[:, h, g * 2 * P + u : (g + 1) * 2 * P : 2], ident_f[:]
+                    )
             nc.vector.tensor_copy(
                 out=w_grp_words[:, g, :, :], in_=w_ps[:].rearrange("p u h r -> p (h r) u")
             )
@@ -295,50 +316,138 @@ def tile_full_tmix_params_pb_t_kernel(tc, x, x_v, W_v, v_hid, v2, v0, v_first, o
         )
         transpose_vh(0)
         copy_vh(0)
+        gate(0, 0)
+        gate(0, 1)
 
         def live(n):
             return 0 <= n < N_STEPS
 
-        def refill(n, g):
-            b, s = n // 4, n % 4
-            if s < 3:
-                transpose_x(b, s + 1, g)
-            elif b + 1 < B:
-                transpose_x(b + 1, 0, g)
-                transpose_wrap(b + 1, g)
-
-        for n in range(N_STEPS + 3):
-            if n + X_AHEAD < N_STEPS:
-                load_x(n + X_AHEAD)
-            if n % 4 == 2 and n // 4 + 2 < B:
-                load_seq(n // 4 + 2)
-            if live(n):
+        form_1 = [j for j in range(2) if FORM[j] == 1]
+        form_2 = [j for j in range(2) if FORM[j] == 2]
+        for n in range(N_STEPS - 1):
+            now, nxt, l1, l2, l3 = live(n), live(n + 1), live(n - 1), live(n - 2), live(n - 3)
+            seq_next = n // 2 + 1 if n % 2 == 0 and n // 2 + 1 < B else 0
+            if l2:
+                project(n - 2)
+            if l1:
+                regroup_pool(n - 1, 0)
+            if now and n > 0:
                 mix(n, 0)
-            if live(n - 1):
-                regroup_act(n - 1, 1, NG1, 2 * P)
-                sigmoid(n - 1)
-            if live(n):
-                refill(n, 0)
-                gate(n)
-            if n % 4 == 1 and n // 4 + 1 < B:
-                transpose_vh(n // 4 + 1)
-            if live(n):
-                scale_x(n, 1)
-            if live(n - 3):
-                blend_add(n - 3)
-            if live(n - 1):
-                quantise(n - 1)
-                project(n - 1)
-            if live(n):
-                regroup_pool(n, 0, 0, 2 * P)
-            if live(n - 2):
-                blend_sub(n - 2)
-                blend_mul(n - 2)
-            if live(n + 1):
-                scale_x(n + 1, 0)
-            if n % 4 == 1 and n // 4 + 1 < B:
-                copy_vh(n // 4 + 1)
-            if live(n):
+            if l1:
+                regroup_act(n - 1, 0)
+            if now:
+                sigmoid(n, 0)
+            if l1:
+                regroup_act(n - 1, 1)
+            if nxt:
+                transpose_x(n + 1, 0)
+            if now:
                 mix(n, 1)
-                refill(n, 1)
-                regroup_pool(n, 1, 0, NG1)
+            if nxt:
+                transpose_x(n + 1, 1)
+            if l3:
+                for j in form_2:
+                    sub_2(n - 3, j)
+                store(n - 3)
+            if l2:
+                for j in form_1:
+                    sub_1(n - 2, j)
+            if now:
+                mix(n, 2)
+                sigmoid(n, 1)
+            if nxt:
+                transpose_x(n + 1, 2)
+            if l2:
+                for j in form_1:
+                    mul_1(n - 2, j)
+            if nxt:
+                scale_x(n + 1, 0)
+            if now:
+                mix(n, 3)
+            if nxt:
+                transpose_x(n + 1, 3)
+            if seq_next:
+                transpose_vh(seq_next)
+            if nxt:
+                scale_x(n + 1, 1)
+            if seq_next:
+                copy_vh(seq_next)
+            if nxt:
+                gate(n + 1, 0)
+                gate(n + 1, 1)
+            if l1:
+                regroup_vec(n - 1, 0)
+                regroup_vec(n - 1, 1)
+            if l2:
+                for j in form_2:
+                    own_2(n - 2, j)
+                    mul_2(n - 2, j)
+            if nxt:
+                scale_x(n + 1, 2)
+            if l1:
+                regroup_pool(n - 1, 1)
+            if l2:
+                for j in form_1:
+                    add_1(n - 2, j)
+            if nxt:
+                scale_x(n + 1, 3)
+            if l1:
+                quantise(n - 1)
+            if n + X_BUFS < N_STEPS:
+                load_x(n + X_BUFS)
+            if n % 2 == 1 and n // 2 + 2 < B:
+                load_seq(n // 2 + 2)
+
+        n = N_STEPS - 1
+        project(n - 2)
+        regroup_pool(n - 1, 0)
+        regroup_pool(n - 1, 1)
+        mix(n, 0)
+        regroup_act(n - 1, 0)
+        regroup_act(n - 1, 1)
+        sigmoid(n, 0)
+        sigmoid(n, 1)
+        mix(n, 1)
+        for j in form_2:
+            sub_2(n - 3, j)
+        store(n - 3)
+        for j in form_1:
+            sub_1(n - 2, j)
+        regroup_vec(n - 1, 0)
+        regroup_vec(n - 1, 1)
+        for j in form_2:
+            own_2(n - 2, j)
+        quantise(n - 1)
+        for j in form_1:
+            mul_1(n - 2, j)
+        for j in form_2:
+            mul_2(n - 2, j)
+        mix(n, 2)
+        project(n - 1)
+        regroup_pool(n, 0, L_POOL)
+        regroup_act(n, 0, L_POOL, L_POOL + L_ACT)
+        for j in form_1:
+            add_1(n - 2, j)
+        mix(n, 3)
+        for j in form_2:
+            sub_2(n - 2, j)
+        store(n - 2)
+        for j in range(2):
+            own_2(n - 1, j)
+        regroup_vec(n, 0, L_POOL + L_ACT)
+        for j in range(2):
+            mul_2(n - 1, j)
+        regroup_act(n, 1, 0, L_ACT)
+        regroup_vec(n, 1, L_ACT)
+        quantise(n, (0, 1))
+        for j in range(2):
+            sub_2(n - 1, j)
+        store(n - 1)
+        quantise(n, (1, 2))
+        for j in range(2):
+            mul_2(n, j)
+        project(n)
+        for j in range(2):
+            own_2(n, j)
+            sub_2(n, j, nc.vector)
+            store_half(n, j)

@@ -20,8 +20,8 @@ NT = H // P
 N_STEPS = B * T // H
 X_BUFS = 5
 R_POOL = 256
-R_ACT = 192
-FORM = (1, 2)
+R_ACT = H - R_POOL
+FORM = (1, 1)
 L_POOL = 128
 L_ACT = 192
 
@@ -113,7 +113,7 @@ def tile_full_tmix_params_pb_t_kernel(tc, x, x_v, W_v, v_hid, v2, v0, v_first, o
             dst, src = quad_views(n, g, lo, hi)
             nc.scalar.copy(out=dst, in_=src)
 
-        def regroup_vec(n, g, lo=R_POOL + R_ACT):
+        def regroup_vec(n, g, lo):
             dst, src = quad_views(n, g, lo, H)
             nc.vector.tensor_copy(out=dst, in_=src)
 
@@ -375,9 +375,6 @@ def tile_full_tmix_params_pb_t_kernel(tc, x, x_v, W_v, v_hid, v2, v0, v_first, o
             if nxt:
                 gate(n + 1, 0)
                 gate(n + 1, 1)
-            if l1:
-                regroup_vec(n - 1, 0)
-                regroup_vec(n - 1, 1)
             if l2:
                 for j in form_2:
                     own_2(n - 2, j)
@@ -413,8 +410,6 @@ def tile_full_tmix_params_pb_t_kernel(tc, x, x_v, W_v, v_hid, v2, v0, v_first, o
         store(n - 3)
         for j in form_1:
             sub_1(n - 2, j)
-        regroup_vec(n - 1, 0)
-        regroup_vec(n - 1, 1)
         for j in form_2:
             own_2(n - 2, j)
         quantise(n - 1)

@@ -19,11 +19,8 @@ H = 512
 NT = H // P
 N_STEPS = B * T // H
 X_BUFS = 5
-R_POOL = 256
-R_ACT = H - R_POOL
-FORM = (1, 1)
-L_POOL = 128
-L_ACT = 192
+R_POOL = (192, 320)
+L_ACT = 256
 
 
 def tile_full_tmix_params_pb_t_kernel(tc, x, x_v, W_v, v_hid, v2, v0, v_first, out):
@@ -95,7 +92,7 @@ def tile_full_tmix_params_pb_t_kernel(tc, x, x_v, W_v, v_hid, v2, v0, v_first, o
 
         def grp(n):
             if n not in grp_tiles:
-                grp_tiles[n] = work.tile([P, 2, H, 4], BF16, name="grp", bufs=1, align_bytes=64)
+                grp_tiles[n] = work.tile([P, 2, H, 4], BF16, name="grp", bufs=2, align_bytes=64)
             return grp_tiles[n]
 
         def quad_views(n, g, lo, hi):
@@ -103,13 +100,13 @@ def tile_full_tmix_params_pb_t_kernel(tc, x, x_v, W_v, v_hid, v2, v0, v_first, o
             src = xvp_tiles[n][:, 4 * g : 4 * g + 4, lo:hi].rearrange("p t (c i) -> p c t i", i=4)
             return dst, src
 
-        def regroup_pool(n, g, hi=R_POOL):
+        def regroup_pool(n, g, hi):
             src = xvp_tiles[n][:, 4 * g : 4 * g + 4, 0:hi].rearrange("p t n -> p n t")
             nc.gpsimd.tensor_scalar(
                 out=grp(n)[:, g, 0:hi, :], in0=src, scalar1=1.0, scalar2=0.0, op0=ALU.mult, op1=ALU.add
             )
 
-        def regroup_act(n, g, lo=R_POOL, hi=R_POOL + R_ACT):
+        def regroup_act(n, g, lo, hi):
             dst, src = quad_views(n, g, lo, hi)
             nc.scalar.copy(out=dst, in_=src)
 
@@ -133,23 +130,22 @@ def tile_full_tmix_params_pb_t_kernel(tc, x, x_v, W_v, v_hid, v2, v0, v_first, o
 
         v_tiles = {}
 
-        def project(n):
+        def project(n, j):
             xc, xs = q_tiles[n]
-            for j in range(2):
-                v_ps = psum.tile([P, 2, CO], F32, tag="v", bufs=2, name="v_ps")
-                for i in range(2):
-                    for g in range(2):
-                        c0 = g * H + (2 * j + i) * P
-                        nc.tensor.matmul_mx(
-                            out=v_ps[:, i, :],
-                            lhsT=xc[:, c0 : c0 + P].bitcast(FP8X4),
-                            lhsT_scale=xs[:, c0 : c0 + P],
-                            rhs=w_codes[:, g * CO : (g + 1) * CO].bitcast(FP8X4),
-                            rhs_scale=w_scales[:, g * CO : (g + 1) * CO],
-                            start=(g == 0),
-                            stop=(g == 1),
-                        )
-                v_tiles[(n, j)] = v_ps
+            v_ps = psum.tile([P, 2, CO], F32, tag="v", bufs=2, name="v_ps")
+            for i in range(2):
+                for g in range(2):
+                    c0 = g * H + (2 * j + i) * P
+                    nc.tensor.matmul_mx(
+                        out=v_ps[:, i, :],
+                        lhsT=xc[:, c0 : c0 + P].bitcast(FP8X4),
+                        lhsT_scale=xs[:, c0 : c0 + P],
+                        rhs=w_codes[:, g * CO : (g + 1) * CO].bitcast(FP8X4),
+                        rhs_scale=w_scales[:, g * CO : (g + 1) * CO],
+                        start=(g == 0),
+                        stop=(g == 1),
+                    )
+            v_tiles[(n, j)] = v_ps
 
         g_tiles = {}
 
@@ -192,7 +188,7 @@ def tile_full_tmix_params_pb_t_kernel(tc, x, x_v, W_v, v_hid, v2, v0, v_first, o
             e_tiles[(n, j)] = e_sb
 
         def mul_1(n, j):
-            f_sb = ep.tile([P, 2, CO], F32, name="f_sb", tag="f%d" % j, bufs=2)
+            f_sb = ep.tile([P, 2, CO], F32, name="f_sb", tag="f%d" % j, bufs=3)
             nc.gpsimd.tensor_tensor(out=f_sb[:], in0=e_tiles[(n, j)][:], in1=mix_tiles[(n, j)][:], op=ALU.mult)
             f_tiles[(n, j)] = f_sb
 
@@ -204,7 +200,7 @@ def tile_full_tmix_params_pb_t_kernel(tc, x, x_v, W_v, v_hid, v2, v0, v_first, o
             nc.sync.dma_start(out=dst[n % 2, j], in_=out_half(n, j))
 
         def mul_2(n, j):
-            f_sb = ep.tile([P, 2, CO], F32, name="f_sb", tag="f%d" % j, bufs=2)
+            f_sb = ep.tile([P, 2, CO], F32, name="f_sb", tag="f%d" % j, bufs=3)
             nc.gpsimd.tensor_tensor(out=f_sb[:], in0=mix_tiles[(n, j)][:], in1=v_first_half(n, j), op=ALU.mult)
             f_tiles[(n, j)] = f_sb
 
@@ -322,126 +318,99 @@ def tile_full_tmix_params_pb_t_kernel(tc, x, x_v, W_v, v_hid, v2, v0, v_first, o
         def live(n):
             return 0 <= n < N_STEPS
 
-        form_1 = [j for j in range(2) if FORM[j] == 1]
-        form_2 = [j for j in range(2) if FORM[j] == 2]
         for n in range(N_STEPS - 1):
-            now, nxt, l1, l2, l3 = live(n), live(n + 1), live(n - 1), live(n - 2), live(n - 3)
+            nxt, l1, l2, l3 = live(n + 1), live(n - 1), live(n - 2), live(n - 3)
             seq_next = n // 2 + 1 if n % 2 == 0 and n // 2 + 1 < B else 0
-            if l2:
-                project(n - 2)
             if l1:
-                regroup_pool(n - 1, 0)
-            if now and n > 0:
-                mix(n, 0)
-            if l1:
-                regroup_act(n - 1, 0)
-            if now:
-                sigmoid(n, 0)
-            if l1:
-                regroup_act(n - 1, 1)
-            if nxt:
-                transpose_x(n + 1, 0)
-            if now:
-                mix(n, 1)
-            if nxt:
-                transpose_x(n + 1, 1)
+                regroup_pool(n - 1, 0, R_POOL[0])
+                regroup_act(n - 1, 0, R_POOL[0], H)
             if l3:
-                for j in form_2:
-                    sub_2(n - 3, j)
+                mul_1(n - 3, 0)
+                mul_1(n - 3, 1)
+            if n > 0:
+                mix(n, 0)
+            transpose_x(n + 1, 0)
+            sigmoid(n, 0)
+            if l1:
+                regroup_act(n - 1, 1, R_POOL[1], H)
+                regroup_pool(n - 1, 1, R_POOL[1])
+            mix(n, 1)
+            transpose_x(n + 1, 1)
+            sigmoid(n, 1)
+            scale_x(n + 1, 0)
+            if l3:
+                add_1(n - 3, 0)
+            if l2:
+                project(n - 2, 0)
+            mix(n, 2)
+            transpose_x(n + 1, 2)
+            scale_x(n + 1, 1)
+            if l3:
+                add_1(n - 3, 1)
                 store(n - 3)
             if l2:
-                for j in form_1:
-                    sub_1(n - 2, j)
-            if now:
-                mix(n, 2)
-                sigmoid(n, 1)
-            if nxt:
-                transpose_x(n + 1, 2)
-            if l2:
-                for j in form_1:
-                    mul_1(n - 2, j)
-            if nxt:
-                scale_x(n + 1, 0)
-            if now:
-                mix(n, 3)
-            if nxt:
-                transpose_x(n + 1, 3)
+                project(n - 2, 1)
+            gate(n + 1, 0)
+            mix(n, 3)
+            transpose_x(n + 1, 3)
+            scale_x(n + 1, 2)
             if seq_next:
                 transpose_vh(seq_next)
-            if nxt:
-                scale_x(n + 1, 1)
+            scale_x(n + 1, 3)
             if seq_next:
                 copy_vh(seq_next)
-            if nxt:
-                gate(n + 1, 0)
-                gate(n + 1, 1)
-            if l2:
-                for j in form_2:
-                    own_2(n - 2, j)
-                    mul_2(n - 2, j)
-            if nxt:
-                scale_x(n + 1, 2)
-            if l1:
-                regroup_pool(n - 1, 1)
-            if l2:
-                for j in form_1:
-                    add_1(n - 2, j)
-            if nxt:
-                scale_x(n + 1, 3)
+            gate(n + 1, 1)
             if l1:
                 quantise(n - 1)
+            if l2:
+                sub_1(n - 2, 0)
+                sub_1(n - 2, 1)
             if n + X_BUFS < N_STEPS:
                 load_x(n + X_BUFS)
             if n % 2 == 1 and n // 2 + 2 < B:
                 load_seq(n // 2 + 2)
 
         n = N_STEPS - 1
-        project(n - 2)
-        regroup_pool(n - 1, 0)
-        regroup_pool(n - 1, 1)
+        regroup_pool(n - 1, 0, R_POOL[0])
+        regroup_act(n - 1, 0, R_POOL[0], H)
+        for j in range(2):
+            mul_1(n - 3, j)
         mix(n, 0)
-        regroup_act(n - 1, 0)
-        regroup_act(n - 1, 1)
+        regroup_act(n - 1, 1, R_POOL[1], H)
+        regroup_pool(n - 1, 1, R_POOL[1])
+        mix(n, 1)
         sigmoid(n, 0)
         sigmoid(n, 1)
-        mix(n, 1)
-        for j in form_2:
-            sub_2(n - 3, j)
+        for j in range(2):
+            add_1(n - 3, j)
+            project(n - 2, j)
         store(n - 3)
-        for j in form_1:
-            sub_1(n - 2, j)
-        for j in form_2:
-            own_2(n - 2, j)
-        quantise(n - 1)
-        for j in form_1:
-            mul_1(n - 2, j)
-        for j in form_2:
-            mul_2(n - 2, j)
+        mul_2(n - 2, 0)
         mix(n, 2)
-        project(n - 1)
-        regroup_pool(n, 0, L_POOL)
-        regroup_act(n, 0, L_POOL, L_POOL + L_ACT)
-        for j in form_1:
-            add_1(n - 2, j)
+        quantise(n - 1)
+        regroup_act(n, 0, 0, H)
         mix(n, 3)
-        for j in form_2:
+        mul_2(n - 2, 1)
+        for j in range(2):
+            own_2(n - 2, j)
+            project(n - 1, j)
+        regroup_act(n, 1, 0, L_ACT)
+        regroup_vec(n, 1, L_ACT)
+        for j in range(2):
+            mul_2(n - 1, j)
+        quantise(n, (0, 1))
+        quantise(n, (1, 2))
+        for j in range(2):
+            own_2(n - 1, j)
+            project(n, j)
+        for j in range(2):
+            mul_2(n, j)
+        for j in range(2):
             sub_2(n - 2, j)
         store(n - 2)
         for j in range(2):
-            own_2(n - 1, j)
-        regroup_vec(n, 0, L_POOL + L_ACT)
-        for j in range(2):
-            mul_2(n - 1, j)
-        regroup_act(n, 1, 0, L_ACT)
-        regroup_vec(n, 1, L_ACT)
-        quantise(n, (0, 1))
-        for j in range(2):
-            sub_2(n - 1, j)
+            sub_2(n - 1, j, nc.vector)
         store(n - 1)
-        quantise(n, (1, 2))
-        for j in range(2):
-            mul_2(n, j)
-        project(n)
         for j in range(2):
             own_2(n, j)
             sub_2(n, j, nc.vector)

@@ -19,8 +19,7 @@ H = 512
 NT = H // P
 N_STEPS = B * T // H
 X_BUFS = 5
-R_POOL = (192, 320)
-L_ACT = 256
+R_POOL = (256, 384)
 
 
 def tile_full_tmix_params_pb_t_kernel(tc, x, x_v, W_v, v_hid, v2, v0, v_first, out):
@@ -39,12 +38,15 @@ def tile_full_tmix_params_pb_t_kernel(tc, x, x_v, W_v, v_hid, v2, v0, v_first, o
         def load_x(n):
             x_sb = xin.tile([P, NT, C], BF16, name="x_sb")
             src = x[n // 2].rearrange("(h i p) c -> h p i c", h=2, p=P)
-            if n == 0:
-                for c0 in (0, C // 2):
-                    nc.sync.dma_start(out=x_sb[:, :, c0 : c0 + C // 2], in_=src[0, :, :, c0 : c0 + C // 2])
-            else:
-                nc.sync.dma_start(out=x_sb[:], in_=src[n % 2])
+            nc.sync.dma_start(out=x_sb[:], in_=src[n % 2])
             x_tiles[n] = x_sb
+
+        def load_x_half(n, q):
+            if q == 0:
+                x_tiles[n] = xin.tile([P, NT, C], BF16, name="x_sb")
+            src = x[n // 2].rearrange("(h i p) (q c) -> h q p i c", h=2, p=P, q=2)
+            c0 = q * C // 2
+            nc.sync.dma_start(out=x_tiles[n][:, :, c0 : c0 + C // 2], in_=src[n % 2, q])
 
         seq_tiles = {}
 
@@ -110,10 +112,6 @@ def tile_full_tmix_params_pb_t_kernel(tc, x, x_v, W_v, v_hid, v2, v0, v_first, o
             dst, src = quad_views(n, g, lo, hi)
             nc.scalar.copy(out=dst, in_=src)
 
-        def regroup_vec(n, g, lo):
-            dst, src = quad_views(n, g, lo, H)
-            nc.vector.tensor_copy(out=dst, in_=src)
-
         q_tiles = {}
 
         def quantise(n, halves=(0, 2)):
@@ -130,9 +128,9 @@ def tile_full_tmix_params_pb_t_kernel(tc, x, x_v, W_v, v_hid, v2, v0, v_first, o
 
         v_tiles = {}
 
-        def project(n, j):
+        def project(n, j, tag="v", bufs=2):
             xc, xs = q_tiles[n]
-            v_ps = psum.tile([P, 2, CO], F32, tag="v", bufs=2, name="v_ps")
+            v_ps = psum.tile([P, 2, CO], F32, tag=tag, bufs=bufs, name="v_ps")
             for i in range(2):
                 for g in range(2):
                     c0 = g * H + (2 * j + i) * P
@@ -243,16 +241,19 @@ def tile_full_tmix_params_pb_t_kernel(tc, x, x_v, W_v, v_hid, v2, v0, v_first, o
         nc.sync.dma_start(
             out=xv_rows[:].bitcast(BF16)[0:2, :], in_=x_v.rearrange("a b (r c) -> (a b r) c", r=2)
         )
-        load_x(0)
+        warm = const.tile([P, 1], F32, name="warm")
+        nc.scalar.activation(out=warm[:], in_=xv_rows[:, P : P + 1], func=ACT.Sigmoid)
+        load_x_half(0, 0)
         w_sb = const.tile([P, 2, C], BF16, name="w_sb")
         nc.sync.dma_start(out=w_sb[:], in_=W_v.rearrange("(h p) c -> p h c", p=P))
+        load_x_half(0, 1)
         v0_rows = const.tile([P, P], BF16, name="v0_rows")
         nc.vector.memset(v0_rows[:], 0.0)
         nc.sync.dma_start(out=v0_rows[0:2, :], in_=v0.rearrange("a b (h c) -> (a b h) c", h=2))
         v2_sb = const.tile([P, CO], BF16, name="v2_sb")
         nc.sync.dma_start(out=v2_sb[:], in_=v2)
-        load_seq(0)
         load_x(1)
+        load_seq(0)
         load_x(2)
         load_seq(1)
         for n in range(3, X_BUFS):
@@ -278,18 +279,10 @@ def tile_full_tmix_params_pb_t_kernel(tc, x, x_v, W_v, v_hid, v2, v0, v_first, o
         nc.vector.tensor_scalar(
             out=om[:], in0=m[:], scalar1=-1.0, scalar2=1.0, op0=ALU.mult, op1=ALU.add
         )
-        for k in range(4):
-            transpose_x(0, k)
-        for k in range(4):
-            scale_x(0, k)
-        mix(0, 0)
-
-        v0_ps = psum.tile([P, P], BF16, tag="g", bufs=2, name="v0_ps")
-        nc.tensor.transpose(v0_ps[:], v0_rows[:], ident_b[:])
-        v0_col = const.tile([P, 2], F32, name="v0_col")
-        nc.vector.tensor_copy(out=v0_col[:], in_=v0_ps[:, 0:2])
-        v0_wide = const.tile([P, 2, P], F32, name="v0_wide")
-        nc.vector.tensor_copy(out=v0_wide[:], in_=v0_col[:].unsqueeze(2).to_broadcast([P, 2, P]))
+        transpose_x(0, 0)
+        transpose_x(0, 1)
+        scale_x(0, 0)
+        scale_x(0, 1)
 
         w_words = w_sb[:].bitcast(F32)
         w_grp = const.tile([P, 2, CO, 4], BF16, name="w_grp", align_bytes=64)
@@ -304,36 +297,59 @@ def tile_full_tmix_params_pb_t_kernel(tc, x, x_v, W_v, v_hid, v2, v0, v_first, o
             nc.vector.tensor_copy(
                 out=w_grp_words[:, g, :, :], in_=w_ps[:].rearrange("p u h r -> p (h r) u")
             )
+        transpose_x(0, 2)
+        transpose_x(0, 3)
+        scale_x(0, 2)
+        scale_x(0, 3)
+        mix(0, 0)
         w_codes = const.tile([P, 2 * CO], U32, name="w_codes", align_bytes=64)
         w_scales = const.tile([P, 2 * CO], U8, name="w_scales", align_bytes=64)
         nc.vector.quantize_mx(
             out=w_codes[:].bitcast(FP8X4), scales=w_scales[:],
             in_=w_grp[:].rearrange("p g c t -> p (g c t)"),
         )
+        mix(0, 1)
+
+        v0_ps = psum.tile([P, P], BF16, tag="g", bufs=2, name="v0_ps")
+        nc.tensor.transpose(v0_ps[:], v0_rows[:], ident_b[:])
+        v0_col = const.tile([P, 2], F32, name="v0_col")
+        nc.vector.tensor_copy(out=v0_col[:], in_=v0_ps[:, 0:2])
+        v0_wide = const.tile([P, 2, P], F32, name="v0_wide")
+        nc.vector.tensor_copy(out=v0_wide[:], in_=v0_col[:].unsqueeze(2).to_broadcast([P, 2, P]))
+        transpose_x(1, 0)
+        transpose_x(1, 1)
+        mix(0, 2)
+        scale_x(1, 0)
         transpose_vh(0)
+        scale_x(1, 1)
+        mix(0, 3)
+        transpose_x(1, 2)
         copy_vh(0)
-        gate(0, 0)
-        gate(0, 1)
+        scale_x(1, 2)
+        transpose_x(1, 3)
+        scale_x(1, 3)
+        for j in range(2):
+            gate(0, j)
+            sigmoid(0, j)
+        transpose_vh(1)
+        gate(1, 0)
+        copy_vh(1)
+        gate(1, 1)
+        load_x(X_BUFS)
 
-        def live(n):
-            return 0 <= n < N_STEPS
-
-        for n in range(N_STEPS - 1):
-            nxt, l1, l2, l3 = live(n + 1), live(n - 1), live(n - 2), live(n - 3)
+        for n in range(1, N_STEPS - 1):
+            l2, l3 = n >= 2, n >= 3
             seq_next = n // 2 + 1 if n % 2 == 0 and n // 2 + 1 < B else 0
-            if l1:
-                regroup_pool(n - 1, 0, R_POOL[0])
-                regroup_act(n - 1, 0, R_POOL[0], H)
+            regroup_pool(n - 1, 0, R_POOL[0])
+            regroup_act(n - 1, 0, R_POOL[0], H)
             if l3:
                 mul_1(n - 3, 0)
                 mul_1(n - 3, 1)
-            if n > 0:
-                mix(n, 0)
+            mix(n, 0)
             transpose_x(n + 1, 0)
             sigmoid(n, 0)
-            if l1:
-                regroup_act(n - 1, 1, R_POOL[1], H)
-                regroup_pool(n - 1, 1, R_POOL[1])
+            regroup_act(n - 1, 1, R_POOL[1], H)
+            regroup_pool(n - 1, 1, R_POOL[1])
             mix(n, 1)
             transpose_x(n + 1, 1)
             sigmoid(n, 1)
@@ -350,18 +366,17 @@ def tile_full_tmix_params_pb_t_kernel(tc, x, x_v, W_v, v_hid, v2, v0, v_first, o
                 store(n - 3)
             if l2:
                 project(n - 2, 1)
+            if seq_next:
+                transpose_vh(seq_next)
             gate(n + 1, 0)
             mix(n, 3)
             transpose_x(n + 1, 3)
             scale_x(n + 1, 2)
             if seq_next:
-                transpose_vh(seq_next)
-            scale_x(n + 1, 3)
-            if seq_next:
                 copy_vh(seq_next)
+            scale_x(n + 1, 3)
             gate(n + 1, 1)
-            if l1:
-                quantise(n - 1)
+            quantise(n - 1)
             if l2:
                 sub_1(n - 2, 0)
                 sub_1(n - 2, 1)
@@ -376,42 +391,42 @@ def tile_full_tmix_params_pb_t_kernel(tc, x, x_v, W_v, v_hid, v2, v0, v_first, o
         for j in range(2):
             mul_1(n - 3, j)
         mix(n, 0)
-        regroup_act(n - 1, 1, R_POOL[1], H)
-        regroup_pool(n - 1, 1, R_POOL[1])
+        regroup_act(n - 1, 1, 0, H)
         mix(n, 1)
-        sigmoid(n, 0)
-        sigmoid(n, 1)
+        regroup_act(n, 0, 0, H)
+        mix(n, 2)
+        mix(n, 3)
+        for j in range(2):
+            mul_2(n - 2, j)
         for j in range(2):
             add_1(n - 3, j)
             project(n - 2, j)
         store(n - 3)
-        mul_2(n - 2, 0)
-        mix(n, 2)
+        mul_2(n - 1, 0)
         quantise(n - 1)
-        regroup_act(n, 0, 0, H)
-        mix(n, 3)
-        mul_2(n - 2, 1)
         for j in range(2):
-            own_2(n - 2, j)
-            project(n - 1, j)
-        regroup_act(n, 1, 0, L_ACT)
-        regroup_vec(n, 1, L_ACT)
+            project(n - 1, j, "xt", 4)
+        regroup_act(n, 1, 0, H)
+        mul_2(n - 1, 1)
         for j in range(2):
-            mul_2(n - 1, j)
+            sigmoid(n, j)
+        own_2(n - 2, 0)
         quantise(n, (0, 1))
+        own_2(n - 2, 1)
         quantise(n, (1, 2))
         for j in range(2):
-            own_2(n - 1, j)
-            project(n, j)
+            project(n, j, "xt", 4)
         for j in range(2):
             mul_2(n, j)
         for j in range(2):
-            sub_2(n - 2, j)
+            own_2(n - 1, j)
+        for j in range(2):
+            sub_2(n - 2, j, nc.vector)
         store(n - 2)
         for j in range(2):
             sub_2(n - 1, j, nc.vector)
+            own_2(n, j)
         store(n - 1)
         for j in range(2):
-            own_2(n, j)
             sub_2(n, j, nc.vector)
             store_half(n, j)

@@ -39,14 +39,15 @@ def tile_full_tmix_params_pb_t_kernel(tc, x, x_v, W_v, v_hid, v2, v0, v_first, o
             x_sb = xin.tile([P, NT, C], BF16, name="x_sb")
             src = x[n // 2].rearrange("(h i p) c -> h p i c", h=2, p=P)
             nc.sync.dma_start(out=x_sb[:], in_=src[n % 2])
-            x_tiles[n] = x_sb
+            x_tiles[n] = x_sb[:].rearrange("p i (g c) -> p g i c", g=2)
 
-        def load_x_half(n, q):
-            if q == 0:
-                x_tiles[n] = xin.tile([P, NT, C], BF16, name="x_sb")
-            src = x[n // 2].rearrange("(h i p) (q c) -> h q p i c", h=2, p=P, q=2)
-            c0 = q * C // 2
-            nc.sync.dma_start(out=x_tiles[n][:, :, c0 : c0 + C // 2], in_=src[n % 2, q])
+        def load_x_first():
+            x_sb = xin.tile([P, NT, C], BF16, name="x_sb")
+            halves = x_sb[:].rearrange("p i c -> p (i c)").rearrange("p (g i c) -> p g i c", g=2, i=NT)
+            src = x[0].rearrange("(h i p) (g c) -> h g p i c", h=2, p=P, g=2)
+            for g in range(2):
+                nc.sync.dma_start(out=halves[:, g, :, :], in_=src[0, g])
+            x_tiles[0] = halves
 
         seq_tiles = {}
 
@@ -61,10 +62,10 @@ def tile_full_tmix_params_pb_t_kernel(tc, x, x_v, W_v, v_hid, v2, v0, v_first, o
 
         def transpose_x(n, k):
             g, u = k // 2, k % 2
-            xw = x_tiles[n][:].bitcast(F32)
             bk = psum.tile([P, NT, P], F32, tag="xt", bufs=4, name="xt_ps")
             for i in range(NT):
-                nc.tensor.transpose(bk[:, i, :], xw[:, i, g * 2 * P + u : (g + 1) * 2 * P : 2], ident_f[:])
+                words = x_tiles[n][:, g, i, :].bitcast(F32)
+                nc.tensor.transpose(bk[:, i, :], words[:, u : 2 * P : 2], ident_f[:])
             banks[(n, k)] = bk[:].bitcast(BF16).rearrange("p i (r e) -> p (i r) e", e=2)
 
         def scale_x(n, k):
@@ -117,8 +118,8 @@ def tile_full_tmix_params_pb_t_kernel(tc, x, x_v, W_v, v_hid, v2, v0, v_first, o
         def quantise(n, halves=(0, 2)):
             lo, hi = halves
             if lo == 0:
-                xc = work.tile([P, 2 * H], U32, name="xc", align_bytes=64)
-                xs = work.tile([P, 2 * H], U8, name="xs", align_bytes=64)
+                xc = work.tile([P, 2 * H], U32, name="xc", bufs=3, align_bytes=64)
+                xs = work.tile([P, 2 * H], U8, name="xs", bufs=3, align_bytes=64)
                 q_tiles[n] = (xc, xs)
             xc, xs = q_tiles[n]
             nc.vector.quantize_mx(
@@ -147,9 +148,9 @@ def tile_full_tmix_params_pb_t_kernel(tc, x, x_v, W_v, v_hid, v2, v0, v_first, o
 
         g_tiles = {}
 
-        def gate(n, j):
+        def gate(n, j, tag="g", bufs=2):
             vht = vht_tiles[n // 2]
-            g_ps = psum.tile([P, 2, CO], F32, tag="g", bufs=2, name="g_ps")
+            g_ps = psum.tile([P, 2, CO], F32, tag=tag, bufs=bufs, name="g_ps")
             for i in range(2):
                 for h in range(2):
                     nc.tensor.matmul(
@@ -186,7 +187,7 @@ def tile_full_tmix_params_pb_t_kernel(tc, x, x_v, W_v, v_hid, v2, v0, v_first, o
             e_tiles[(n, j)] = e_sb
 
         def mul_1(n, j):
-            f_sb = ep.tile([P, 2, CO], F32, name="f_sb", tag="f%d" % j, bufs=3)
+            f_sb = ep.tile([P, 2, CO], F32, name="f_sb", tag="f%d" % j, bufs=2)
             nc.gpsimd.tensor_tensor(out=f_sb[:], in0=e_tiles[(n, j)][:], in1=mix_tiles[(n, j)][:], op=ALU.mult)
             f_tiles[(n, j)] = f_sb
 
@@ -198,7 +199,7 @@ def tile_full_tmix_params_pb_t_kernel(tc, x, x_v, W_v, v_hid, v2, v0, v_first, o
             nc.sync.dma_start(out=dst[n % 2, j], in_=out_half(n, j))
 
         def mul_2(n, j):
-            f_sb = ep.tile([P, 2, CO], F32, name="f_sb", tag="f%d" % j, bufs=3)
+            f_sb = ep.tile([P, 2, CO], F32, name="f_sb", tag="f%d" % j, bufs=2)
             nc.gpsimd.tensor_tensor(out=f_sb[:], in0=mix_tiles[(n, j)][:], in1=v_first_half(n, j), op=ALU.mult)
             f_tiles[(n, j)] = f_sb
 
@@ -236,24 +237,24 @@ def tile_full_tmix_params_pb_t_kernel(tc, x, x_v, W_v, v_hid, v2, v0, v_first, o
             )
             vht_tiles[b] = vht
 
+        warm = const.tile([P, 1], F32, name="warm")
+        nc.vector.memset(warm[:], 0.0)
+        nc.scalar.activation(out=warm[:], in_=warm[:], func=ACT.Sigmoid)
         xv_rows = const.tile([P, 2 * P], F32, name="xv_rows")
         nc.vector.memset(xv_rows[:], 0.0)
         nc.sync.dma_start(
             out=xv_rows[:].bitcast(BF16)[0:2, :], in_=x_v.rearrange("a b (r c) -> (a b r) c", r=2)
         )
-        warm = const.tile([P, 1], F32, name="warm")
-        nc.scalar.activation(out=warm[:], in_=xv_rows[:, P : P + 1], func=ACT.Sigmoid)
-        load_x_half(0, 0)
-        w_sb = const.tile([P, 2, C], BF16, name="w_sb")
-        nc.sync.dma_start(out=w_sb[:], in_=W_v.rearrange("(h p) c -> p h c", p=P))
-        load_x_half(0, 1)
+        load_x_first()
         v0_rows = const.tile([P, P], BF16, name="v0_rows")
         nc.vector.memset(v0_rows[:], 0.0)
         nc.sync.dma_start(out=v0_rows[0:2, :], in_=v0.rearrange("a b (h c) -> (a b h) c", h=2))
-        v2_sb = const.tile([P, CO], BF16, name="v2_sb")
-        nc.sync.dma_start(out=v2_sb[:], in_=v2)
         load_x(1)
         load_seq(0)
+        w_sb = const.tile([P, 2, C], BF16, name="w_sb")
+        nc.sync.dma_start(out=w_sb[:], in_=W_v.rearrange("(h p) c -> p h c", p=P))
+        v2_sb = const.tile([P, CO], BF16, name="v2_sb")
+        nc.sync.dma_start(out=v2_sb[:], in_=v2)
         load_x(2)
         load_seq(1)
         for n in range(3, X_BUFS):
@@ -279,14 +280,28 @@ def tile_full_tmix_params_pb_t_kernel(tc, x, x_v, W_v, v_hid, v2, v0, v_first, o
         nc.vector.tensor_scalar(
             out=om[:], in0=m[:], scalar1=-1.0, scalar2=1.0, op0=ALU.mult, op1=ALU.add
         )
-        transpose_x(0, 0)
-        transpose_x(0, 1)
-        scale_x(0, 0)
-        scale_x(0, 1)
 
+        for k in range(4):
+            transpose_x(0, k)
+            scale_x(0, k)
+        v0_ps = psum.tile([P, P], BF16, tag="g", bufs=2, name="v0_ps")
+        nc.tensor.transpose(v0_ps[:], v0_rows[:], ident_b[:])
+        v0_col = const.tile([P, 2], F32, name="v0_col")
+        nc.vector.tensor_copy(out=v0_col[:], in_=v0_ps[:, 0:2])
+        v0_wide = const.tile([P, 2, P], F32, name="v0_wide")
+        nc.vector.tensor_copy(out=v0_wide[:], in_=v0_col[:].unsqueeze(2).to_broadcast([P, 2, P]))
+        for k in range(4):
+            mix(0, k)
+            transpose_x(1, k)
+            scale_x(1, k)
+        for g in range(2):
+            regroup_pool(0, g, H)
+        transpose_vh(0)
+        copy_vh(0)
         w_words = w_sb[:].bitcast(F32)
         w_grp = const.tile([P, 2, CO, 4], BF16, name="w_grp", align_bytes=64)
         w_grp_words = w_grp[:].bitcast(F32)
+        w_banks = []
         for g in range(2):
             w_ps = psum.tile([P, 2, 2, P], F32, tag="v", bufs=2, name="w_ps")
             for u in range(2):
@@ -294,92 +309,114 @@ def tile_full_tmix_params_pb_t_kernel(tc, x, x_v, W_v, v_hid, v2, v0, v_first, o
                     nc.tensor.transpose(
                         w_ps[:, u, h, :], w_words[:, h, g * 2 * P + u : (g + 1) * 2 * P : 2], ident_f[:]
                     )
+            w_banks.append(w_ps)
+        for k in range(4):
+            mix(1, k)
+            transpose_x(2, k)
+            scale_x(2, k)
+        quantise(0)
+        regroup_pool(1, 0, R_POOL[0])
+        regroup_pool(1, 1, H)
+        for j in range(2):
+            gate(0, j)
+            sigmoid(0, j)
+        regroup_act(1, 0, R_POOL[0], H)
+        for g in range(2):
             nc.vector.tensor_copy(
-                out=w_grp_words[:, g, :, :], in_=w_ps[:].rearrange("p u h r -> p (h r) u")
+                out=w_grp_words[:, g, :, :], in_=w_banks[g][:].rearrange("p u h r -> p (h r) u")
             )
-        transpose_x(0, 2)
-        transpose_x(0, 3)
-        scale_x(0, 2)
-        scale_x(0, 3)
-        mix(0, 0)
+        for k in range(4):
+            mix(2, k)
+            transpose_x(3, k)
+            scale_x(3, k)
+            if k in (1, 2):
+                gate(1, k - 1)
+                sigmoid(1, k - 1)
+        transpose_vh(1)
+        copy_vh(1)
         w_codes = const.tile([P, 2 * CO], U32, name="w_codes", align_bytes=64)
         w_scales = const.tile([P, 2 * CO], U8, name="w_scales", align_bytes=64)
+        quantise(1)
         nc.vector.quantize_mx(
             out=w_codes[:].bitcast(FP8X4), scales=w_scales[:],
             in_=w_grp[:].rearrange("p g c t -> p (g c t)"),
         )
-        mix(0, 1)
+        for n in range(X_BUFS, X_BUFS + 3):
+            load_x(n)
+        load_seq(2)
 
-        v0_ps = psum.tile([P, P], BF16, tag="g", bufs=2, name="v0_ps")
-        nc.tensor.transpose(v0_ps[:], v0_rows[:], ident_b[:])
-        v0_col = const.tile([P, 2], F32, name="v0_col")
-        nc.vector.tensor_copy(out=v0_col[:], in_=v0_ps[:, 0:2])
-        v0_wide = const.tile([P, 2, P], F32, name="v0_wide")
-        nc.vector.tensor_copy(out=v0_wide[:], in_=v0_col[:].unsqueeze(2).to_broadcast([P, 2, P]))
-        transpose_x(1, 0)
-        transpose_x(1, 1)
-        mix(0, 2)
-        scale_x(1, 0)
-        transpose_vh(0)
-        scale_x(1, 1)
-        mix(0, 3)
-        transpose_x(1, 2)
-        copy_vh(0)
-        scale_x(1, 2)
-        transpose_x(1, 3)
-        scale_x(1, 3)
+        for g in range(2):
+            regroup_pool(2, g, R_POOL[g])
+            regroup_act(2, g, R_POOL[g], H)
         for j in range(2):
-            gate(0, j)
-            sigmoid(0, j)
-        transpose_vh(1)
-        gate(1, 0)
-        copy_vh(1)
-        gate(1, 1)
-        load_x(X_BUFS)
+            mul_2(0, j)
+            project(0, j)
+        mix(3, 0)
+        transpose_x(4, 0)
+        scale_x(4, 0)
+        mix(3, 1)
+        transpose_x(4, 1)
+        scale_x(4, 1)
+        gate(2, 0)
+        sigmoid(2, 0)
+        mix(3, 2)
+        transpose_x(4, 2)
+        scale_x(4, 2)
+        own_2(0, 0)
+        project(1, 0)
+        own_2(0, 1)
+        project(1, 1)
+        mix(3, 3)
+        transpose_x(4, 3)
+        scale_x(4, 3)
+        gate(2, 1)
+        sigmoid(2, 1)
+        for j in range(2):
+            gate(3, j)
+        quantise(2)
+        for j in range(2):
+            sub_2(0, j)
+        store(0)
+        for j in range(2):
+            sub_1(1, j)
+        load_x(X_BUFS + 3)
+        load_seq(3)
 
-        for n in range(1, N_STEPS - 1):
-            l2, l3 = n >= 2, n >= 3
-            seq_next = n // 2 + 1 if n % 2 == 0 and n // 2 + 1 < B else 0
+        for n in range(4, N_STEPS - 1):
             regroup_pool(n - 1, 0, R_POOL[0])
             regroup_act(n - 1, 0, R_POOL[0], H)
-            if l3:
-                mul_1(n - 3, 0)
-                mul_1(n - 3, 1)
+            mul_1(n - 3, 0)
+            mul_1(n - 3, 1)
             mix(n, 0)
             transpose_x(n + 1, 0)
-            sigmoid(n, 0)
+            sigmoid(n - 1, 0)
             regroup_act(n - 1, 1, R_POOL[1], H)
             regroup_pool(n - 1, 1, R_POOL[1])
             mix(n, 1)
             transpose_x(n + 1, 1)
-            sigmoid(n, 1)
+            sigmoid(n - 1, 1)
             scale_x(n + 1, 0)
-            if l3:
-                add_1(n - 3, 0)
-            if l2:
-                project(n - 2, 0)
+            add_1(n - 3, 0)
+            project(n - 2, 0)
+            if n % 2 == 0:
+                transpose_vh(n // 2)
             mix(n, 2)
             transpose_x(n + 1, 2)
             scale_x(n + 1, 1)
-            if l3:
-                add_1(n - 3, 1)
-                store(n - 3)
-            if l2:
-                project(n - 2, 1)
-            if seq_next:
-                transpose_vh(seq_next)
-            gate(n + 1, 0)
+            add_1(n - 3, 1)
+            store(n - 3)
+            project(n - 2, 1)
+            scale_x(n + 1, 2)
+            if n % 2 == 0:
+                copy_vh(n // 2)
             mix(n, 3)
             transpose_x(n + 1, 3)
-            scale_x(n + 1, 2)
-            if seq_next:
-                copy_vh(seq_next)
             scale_x(n + 1, 3)
-            gate(n + 1, 1)
+            gate(n, 0)
+            gate(n, 1)
             quantise(n - 1)
-            if l2:
-                sub_1(n - 2, 0)
-                sub_1(n - 2, 1)
+            sub_1(n - 2, 0)
+            sub_1(n - 2, 1)
             if n + X_BUFS < N_STEPS:
                 load_x(n + X_BUFS)
             if n % 2 == 1 and n // 2 + 2 < B:
@@ -391,8 +428,12 @@ def tile_full_tmix_params_pb_t_kernel(tc, x, x_v, W_v, v_hid, v2, v0, v_first, o
         for j in range(2):
             mul_1(n - 3, j)
         mix(n, 0)
+        gate(n, 0, "xt", 4)
+        for j in range(2):
+            sigmoid(n - 1, j)
         regroup_act(n - 1, 1, 0, H)
         mix(n, 1)
+        gate(n, 1, "xt", 4)
         regroup_act(n, 0, 0, H)
         mix(n, 2)
         mix(n, 3)
@@ -406,27 +447,28 @@ def tile_full_tmix_params_pb_t_kernel(tc, x, x_v, W_v, v_hid, v2, v0, v_first, o
         quantise(n - 1)
         for j in range(2):
             project(n - 1, j, "xt", 4)
-        regroup_act(n, 1, 0, H)
         mul_2(n - 1, 1)
+        regroup_act(n, 1, 0, H)
         for j in range(2):
             sigmoid(n, j)
-        own_2(n - 2, 0)
+        for j in range(2):
+            own_2(n - 2, j)
         quantise(n, (0, 1))
-        own_2(n - 2, 1)
         quantise(n, (1, 2))
         for j in range(2):
             project(n, j, "xt", 4)
         for j in range(2):
-            mul_2(n, j)
+            sub_2(n - 2, j)
+        store(n - 2)
         for j in range(2):
             own_2(n - 1, j)
         for j in range(2):
-            sub_2(n - 2, j, nc.vector)
-        store(n - 2)
-        for j in range(2):
             sub_2(n - 1, j, nc.vector)
-            own_2(n, j)
         store(n - 1)
+        for j in range(2):
+            mul_2(n, j)
+        for j in range(2):
+            own_2(n, j)
         for j in range(2):
             sub_2(n, j, nc.vector)
             store_half(n, j)

@@ -19,7 +19,7 @@ H = 512
 NT = H // P
 N_STEPS = B * T // H
 X_BUFS = 5
-R_POOL = (256, 384)
+R_POOL = (320, 384)
 
 
 def tile_full_tmix_params_pb_t_kernel(tc, x, x_v, W_v, v_hid, v2, v0, v_first, out):
@@ -325,7 +325,14 @@ def tile_full_tmix_params_pb_t_kernel(tc, x, x_v, W_v, v_hid, v2, v0, v_first, o
             nc.vector.tensor_copy(
                 out=w_grp_words[:, g, :, :], in_=w_banks[g][:].rearrange("p u h r -> p (h r) u")
             )
+        w_codes = const.tile([P, 2 * CO], U32, name="w_codes", align_bytes=64)
+        w_scales = const.tile([P, 2 * CO], U8, name="w_scales", align_bytes=64)
         for k in range(4):
+            if k == 2:
+                nc.vector.quantize_mx(
+                    out=w_codes[:].bitcast(FP8X4), scales=w_scales[:],
+                    in_=w_grp[:].rearrange("p g c t -> p (g c t)"),
+                )
             mix(2, k)
             transpose_x(3, k)
             scale_x(3, k)
@@ -334,13 +341,7 @@ def tile_full_tmix_params_pb_t_kernel(tc, x, x_v, W_v, v_hid, v2, v0, v_first, o
                 sigmoid(1, k - 1)
         transpose_vh(1)
         copy_vh(1)
-        w_codes = const.tile([P, 2 * CO], U32, name="w_codes", align_bytes=64)
-        w_scales = const.tile([P, 2 * CO], U8, name="w_scales", align_bytes=64)
         quantise(1)
-        nc.vector.quantize_mx(
-            out=w_codes[:].bitcast(FP8X4), scales=w_scales[:],
-            in_=w_grp[:].rearrange("p g c t -> p (g c t)"),
-        )
         for n in range(X_BUFS, X_BUFS + 3):
             load_x(n)
         load_seq(2)

@@ -19,7 +19,7 @@ H = 512
 NT = H // P
 N_STEPS = B * T // H
 X_BUFS = 5
-R_POOL = (320, 384)
+R_POOL = (256, 384)
 
 
 def tile_full_tmix_params_pb_t_kernel(tc, x, x_v, W_v, v_hid, v2, v0, v_first, out):
@@ -104,10 +104,8 @@ def tile_full_tmix_params_pb_t_kernel(tc, x, x_v, W_v, v_hid, v2, v0, v_first, o
             return dst, src
 
         def regroup_pool(n, g, hi):
-            src = xvp_tiles[n][:, 4 * g : 4 * g + 4, 0:hi].rearrange("p t n -> p n t")
-            nc.gpsimd.tensor_scalar(
-                out=grp(n)[:, g, 0:hi, :], in0=src, scalar1=1.0, scalar2=0.0, op0=ALU.mult, op1=ALU.add
-            )
+            dst, src = quad_views(n, g, 0, hi)
+            nc.gpsimd.tensor_scalar(out=dst, in0=src, scalar1=1.0, scalar2=0.0, op0=ALU.mult, op1=ALU.add)
 
         def regroup_act(n, g, lo, hi):
             dst, src = quad_views(n, g, lo, hi)

@@ -99,8 +99,8 @@ def tile_full_tmix_params_pb_t_kernel(tc, x, x_v, W_v, v_hid, v2, v0, v_first, o
             return grp_tiles[n]
 
         def quad_views(n, g, lo, hi):
-            dst = grp(n)[:, g, lo:hi, :].rearrange("p (c i) t -> p c t i", i=4)
-            src = xvp_tiles[n][:, 4 * g : 4 * g + 4, lo:hi].rearrange("p t (c i) -> p c t i", i=4)
+            dst = grp(n)[:, g, lo:hi, :].rearrange("p (c i) t -> p c t i", i=8)
+            src = xvp_tiles[n][:, 4 * g : 4 * g + 4, lo:hi].rearrange("p t (c i) -> p c t i", i=8)
             return dst, src
 
         def regroup_pool(n, g, hi):

from contextlib import ExitStack

import concourse.mybir as mybir
from concourse.masks import make_identity

FP8X4 = mybir.dt.float8_e4m3fn_x4
BF16 = mybir.dt.bfloat16
F32 = mybir.dt.float32
U32 = mybir.dt.uint32
U8 = mybir.dt.uint8
ALU = mybir.AluOpType
ACT = mybir.ActivationFunctionType

P = 128
B, T, C, CO, DV = 8, 1024, 1024, 256, 128
FLOPS = 2 * B * T * C * CO + 2 * B * T * DV * CO

H = 512
NT = H // P
N_STEPS = B * T // H
X_BUFS = 5
R_POOL = (256, 384)


def tile_full_tmix_params_pb_t_kernel(tc, x, x_v, W_v, v_hid, v2, v0, v_first, out):
    nc = tc.nc
    with ExitStack() as ctx:
        const = ctx.enter_context(tc.tile_pool(name="const", bufs=1))
        xin = ctx.enter_context(tc.tile_pool(name="xin", bufs=X_BUFS))
        seqp = ctx.enter_context(tc.tile_pool(name="seqp", bufs=3))
        work = ctx.enter_context(tc.tile_pool(name="work", bufs=2))
        ep = ctx.enter_context(tc.tile_pool(name="ep", bufs=3))
        psum = ctx.enter_context(tc.psum_pool(name="psum", bufs=1))
        ctx.enter_context(tc.manual_schedule())

        x_tiles = {}

        def load_x(n):
            x_sb = xin.tile([P, NT, C], BF16, name="x_sb")
            src = x[n // 2].rearrange("(h i p) c -> h p i c", h=2, p=P)
            nc.sync.dma_start(out=x_sb[:], in_=src[n % 2])
            x_tiles[n] = x_sb[:].rearrange("p i (g c) -> p g i c", g=2)

        def load_x_first():
            x_sb = xin.tile([P, NT, C], BF16, name="x_sb")
            halves = x_sb[:].rearrange("p i c -> p (i c)").rearrange("p (g i c) -> p g i c", g=2, i=NT)
            src = x[0].rearrange("(h i p) (g c) -> h g p i c", h=2, p=P, g=2)
            for g in range(2):
                nc.sync.dma_start(out=halves[:, g, :, :], in_=src[0, g])
            x_tiles[0] = halves

        seq_tiles = {}

        def load_seq(b):
            vh = seqp.tile([P, 8, DV], BF16, name="vh")
            nc.sync.dma_start(out=vh[:], in_=v_hid[b].rearrange("(p j) d -> p j d", j=8))
            vf = seqp.tile([P, 8, CO], BF16, name="vf")
            nc.sync.dma_start(out=vf[:], in_=v_first[b].rearrange("(i p) c -> p i c", p=P))
            seq_tiles[b] = (vh, vf)

        banks = {}

        def transpose_x(n, k):
            g, u = k // 2, k % 2
            bk = psum.tile([P, NT, P], F32, tag="xt", bufs=4, name="xt_ps")
            for i in range(NT):
                words = x_tiles[n][:, g, i, :].bitcast(F32)
                nc.tensor.transpose(bk[:, i, :], words[:, u : 2 * P : 2], ident_f[:])
            banks[(n, k)] = bk[:].bitcast(BF16).rearrange("p i (r e) -> p (i r) e", e=2)

        def scale_x(n, k):
            a = a_tiles[(n // 2) % 2]
            c0 = 1 + (n % 2) * H
            for e in range(2):
                pl = 2 * k + e
                nc.scalar.activation(
                    out=a[:, pl, c0 : c0 + H], in_=banks[(n, k)][:, :, e], func=ACT.Copy, scale=m[:, pl : pl + 1]
                )

        xvp_tiles = {}

        def mix(n, k):
            a = a_tiles[(n // 2) % 2]
            c0 = (n % 2) * H
            if k == 0:
                xvp_tiles[n] = work.tile([P, 8, H], BF16, name="xvp", bufs=3)
            for e in range(2):
                pl = 2 * k + e
                nc.vector.scalar_tensor_tensor(
                    out=xvp_tiles[n][:, pl, :], in0=banks[(n, k)][:, :, e], scalar=om[:, pl : pl + 1],
                    in1=a[:, pl, c0 : c0 + H], op0=ALU.mult, op1=ALU.add,
                )

        grp_tiles = {}

        def grp(n):
            if n not in grp_tiles:
                grp_tiles[n] = work.tile([P, 2, H, 4], BF16, name="grp", bufs=2, align_bytes=64)
            return grp_tiles[n]

        def quad_views(n, g, lo, hi):
            dst = grp(n)[:, g, lo:hi, :].rearrange("p (c i) t -> p c t i", i=8)
            src = xvp_tiles[n][:, 4 * g : 4 * g + 4, lo:hi].rearrange("p t (c i) -> p c t i", i=8)
            return dst, src

        def regroup_pool(n, g, hi):
            dst, src = quad_views(n, g, 0, hi)
            nc.gpsimd.tensor_scalar(out=dst, in0=src, scalar1=1.0, scalar2=0.0, op0=ALU.mult, op1=ALU.add)

        def regroup_act(n, g, lo, hi):
            dst, src = quad_views(n, g, lo, hi)
            nc.scalar.copy(out=dst, in_=src)

        q_tiles = {}

        def quantise(n, halves=(0, 2)):
            lo, hi = halves
            if lo == 0:
                xc = work.tile([P, 2 * H], U32, name="xc", bufs=3, align_bytes=64)
                xs = work.tile([P, 2 * H], U8, name="xs", bufs=3, align_bytes=64)
                q_tiles[n] = (xc, xs)
            xc, xs = q_tiles[n]
            nc.vector.quantize_mx(
                out=xc[:, lo * H : hi * H].bitcast(FP8X4), scales=xs[:, lo * H : hi * H],
                in_=grp(n)[:, lo:hi].rearrange("p g n t -> p (g n t)"),
            )

        v_tiles = {}

        def project(n, j, tag="v", bufs=2):
            xc, xs = q_tiles[n]
            v_ps = psum.tile([P, 2, CO], F32, tag=tag, bufs=bufs, name="v_ps")
            for i in range(2):
                for g in range(2):
                    c0 = g * H + (2 * j + i) * P
                    nc.tensor.matmul_mx(
                        out=v_ps[:, i, :],
                        lhsT=xc[:, c0 : c0 + P].bitcast(FP8X4),
                        lhsT_scale=xs[:, c0 : c0 + P],
                        rhs=w_codes[:, g * CO : (g + 1) * CO].bitcast(FP8X4),
                        rhs_scale=w_scales[:, g * CO : (g + 1) * CO],
                        start=(g == 0),
                        stop=(g == 1),
                    )
            v_tiles[(n, j)] = v_ps

        g_tiles = {}

        def gate(n, j, tag="g", bufs=2):
            vht = vht_tiles[n // 2]
            g_ps = psum.tile([P, 2, CO], F32, tag=tag, bufs=bufs, name="g_ps")
            for i in range(2):
                for h in range(2):
                    nc.tensor.matmul(
                        out=g_ps[:, i, h * P : (h + 1) * P], lhsT=v0_wide[:, h, :], rhs=ident_f[:],
                        is_transpose=True, start=(h == 0), stop=False,
                    )
                t0 = (n % 2) * H + (2 * j + i) * P
                nc.tensor.matmul(out=g_ps[:, i, :], lhsT=vht[:, t0 : t0 + P], rhs=v2_sb[:], start=False, stop=True)
            g_tiles[(n, j)] = g_ps

        mix_tiles = {}

        def sigmoid(n, j):
            mx_t = ep.tile([P, 2, CO], F32, name="mix_sb", tag="mix%d" % j)
            nc.scalar.activation(out=mx_t[:], in_=g_tiles[(n, j)][:], func=ACT.Sigmoid)
            mix_tiles[(n, j)] = mx_t

        e_tiles = {}
        f_tiles = {}
        o_tiles = {}

        def out_half(n, j):
            if n not in o_tiles:
                o_tiles[n] = ep.tile([P, NT, CO], F32, name="o_sb")
            return o_tiles[n][:, 2 * j : 2 * j + 2, :]

        def v_first_half(n, j):
            i0 = (n % 2) * NT + 2 * j
            return seq_tiles[n // 2][1][:, i0 : i0 + 2, :]

        def sub_1(n, j):
            e_sb = ep.tile([P, 2, CO], F32, name="e_sb", tag="e%d" % j, bufs=2)
            nc.vector.tensor_tensor(out=e_sb[:], in0=v_first_half(n, j), in1=v_tiles[(n, j)][:], op=ALU.subtract)
            e_tiles[(n, j)] = e_sb

        def mul_1(n, j):
            f_sb = ep.tile([P, 2, CO], F32, name="f_sb", tag="f%d" % j, bufs=2)
            nc.gpsimd.tensor_tensor(out=f_sb[:], in0=e_tiles[(n, j)][:], in1=mix_tiles[(n, j)][:], op=ALU.mult)
            f_tiles[(n, j)] = f_sb

        def add_1(n, j):
            nc.vector.tensor_tensor(out=out_half(n, j), in0=f_tiles[(n, j)][:], in1=v_tiles[(n, j)][:], op=ALU.add)

        def store_half(n, j):
            dst = out[n // 2].rearrange("(h j i p) c -> h j p i c", h=2, j=2, p=P)
            nc.sync.dma_start(out=dst[n % 2, j], in_=out_half(n, j))

        def mul_2(n, j):
            f_sb = ep.tile([P, 2, CO], F32, name="f_sb", tag="f%d" % j, bufs=2)
            nc.gpsimd.tensor_tensor(out=f_sb[:], in0=mix_tiles[(n, j)][:], in1=v_first_half(n, j), op=ALU.mult)
            f_tiles[(n, j)] = f_sb

        def own_2(n, j):
            e_sb = ep.tile([P, 2, CO], F32, name="e_sb", tag="e%d" % j, bufs=2)
            nc.vector.scalar_tensor_tensor(
                out=e_sb[:], in0=mix_tiles[(n, j)][:], scalar=1.0, in1=v_tiles[(n, j)][:],
                op0=ALU.subtract, op1=ALU.mult,
            )
            e_tiles[(n, j)] = e_sb

        def sub_2(n, j, eng=nc.gpsimd):
            eng.tensor_tensor(
                out=out_half(n, j), in0=f_tiles[(n, j)][:], in1=e_tiles[(n, j)][:], op=ALU.subtract
            )

        def store(n):
            dst = out[n // 2].rearrange("(h i p) c -> h p i c", h=2, p=P)
            nc.sync.dma_start(out=dst[n % 2], in_=o_tiles[n][:])

        vht_tiles = {}
        vh_banks = {}

        def transpose_vh(b):
            vh = seq_tiles[b][0]
            vh_ps = psum.tile([P, 8, P], BF16, tag="g", bufs=2, name="vh_ps")
            for j in range(8):
                nc.tensor.transpose(vh_ps[:, j, :], vh[:, j, :], ident_b[:])
            vh_banks[b] = vh_ps

        def copy_vh(b):
            vht = seqp.tile([P, T], BF16, name="vht")
            nc.scalar.copy(
                out=vht[:].rearrange("d (p j) -> d p j", j=8), in_=vh_banks[b][:].rearrange("d j p -> d p j")
            )
            vht_tiles[b] = vht

        warm = const.tile([P, 1], F32, name="warm")
        nc.vector.memset(warm[:], 0.0)
        nc.scalar.activation(out=warm[:], in_=warm[:], func=ACT.Sigmoid)
        xv_rows = const.tile([P, 2 * P], F32, name="xv_rows")
        nc.vector.memset(xv_rows[:], 0.0)
        nc.sync.dma_start(
            out=xv_rows[:].bitcast(BF16)[0:2, :], in_=x_v.rearrange("a b (r c) -> (a b r) c", r=2)
        )
        load_x_first()
        v0_rows = const.tile([P, P], BF16, name="v0_rows")
        nc.vector.memset(v0_rows[:], 0.0)
        nc.sync.dma_start(out=v0_rows[0:2, :], in_=v0.rearrange("a b (h c) -> (a b h) c", h=2))
        load_x(1)
        load_seq(0)
        w_sb = const.tile([P, 2, C], BF16, name="w_sb")
        nc.sync.dma_start(out=w_sb[:], in_=W_v.rearrange("(h p) c -> p h c", p=P))
        v2_sb = const.tile([P, CO], BF16, name="v2_sb")
        nc.sync.dma_start(out=v2_sb[:], in_=v2)
        load_x(2)
        load_seq(1)
        for n in range(3, X_BUFS):
            load_x(n)

        ident_f = const.tile([P, P], F32, name="ident_f")
        make_identity(nc, ident_f[:])
        ident_b = const.tile([P, P], BF16, name="ident_b")
        make_identity(nc, ident_b[:])
        a_tiles = []
        for j in range(2):
            a_sb = const.tile([P, 8, 1 + T], F32, name="a%d" % j)
            nc.gpsimd.memset(a_sb[:, :, 0:1], 0.0)
            a_tiles.append(a_sb)

        xv_ps = psum.tile([P, 2, P], F32, tag="g", bufs=2, name="xv_ps")
        for u in range(2):
            nc.tensor.transpose(xv_ps[:, u, :], xv_rows[:, u : 2 * P : 2], ident_f[:])
        m = const.tile([P, 8], F32, name="m")
        xv_planes = xv_ps[:].bitcast(BF16).rearrange("p u (g e) -> p u g e", e=2)[:, :, 0:2, :]
        nc.vector.tensor_copy(out=m[:].rearrange("p (g u e) -> p u g e", g=2, u=2), in_=xv_planes)
        om = const.tile([P, 8], F32, name="om")
        nc.vector.tensor_scalar(
            out=om[:], in0=m[:], scalar1=-1.0, scalar2=1.0, op0=ALU.mult, op1=ALU.add
        )

        for k in range(4):
            transpose_x(0, k)
            scale_x(0, k)
        v0_ps = psum.tile([P, P], BF16, tag="g", bufs=2, name="v0_ps")
        nc.tensor.transpose(v0_ps[:], v0_rows[:], ident_b[:])
        v0_col = const.tile([P, 2], F32, name="v0_col")
        nc.vector.tensor_copy(out=v0_col[:], in_=v0_ps[:, 0:2])
        v0_wide = const.tile([P, 2, P], F32, name="v0_wide")
        nc.vector.tensor_copy(out=v0_wide[:], in_=v0_col[:].unsqueeze(2).to_broadcast([P, 2, P]))
        for k in range(4):
            mix(0, k)
            transpose_x(1, k)
            scale_x(1, k)
        for g in range(2):
            regroup_pool(0, g, H)
        transpose_vh(0)
        copy_vh(0)
        w_words = w_sb[:].bitcast(F32)
        w_grp = const.tile([P, 2, CO, 4], BF16, name="w_grp", align_bytes=64)
        w_grp_words = w_grp[:].bitcast(F32)
        w_banks = []
        for g in range(2):
            w_ps = psum.tile([P, 2, 2, P], F32, tag="v", bufs=2, name="w_ps")
            for u in range(2):
                for h in range(2):
                    nc.tensor.transpose(
                        w_ps[:, u, h, :], w_words[:, h, g * 2 * P + u : (g + 1) * 2 * P : 2], ident_f[:]
                    )
            w_banks.append(w_ps)
        for k in range(4):
            mix(1, k)
            transpose_x(2, k)
            scale_x(2, k)
        quantise(0)
        regroup_pool(1, 0, R_POOL[0])
        regroup_pool(1, 1, H)
        for j in range(2):
            gate(0, j)
            sigmoid(0, j)
        regroup_act(1, 0, R_POOL[0], H)
        for g in range(2):
            nc.vector.tensor_copy(
                out=w_grp_words[:, g, :, :], in_=w_banks[g][:].rearrange("p u h r -> p (h r) u")
            )
        w_codes = const.tile([P, 2 * CO], U32, name="w_codes", align_bytes=64)
        w_scales = const.tile([P, 2 * CO], U8, name="w_scales", align_bytes=64)
        for k in range(4):
            if k == 2:
                nc.vector.quantize_mx(
                    out=w_codes[:].bitcast(FP8X4), scales=w_scales[:],
                    in_=w_grp[:].rearrange("p g c t -> p (g c t)"),
                )
            mix(2, k)
            transpose_x(3, k)
            scale_x(3, k)
            if k in (1, 2):
                gate(1, k - 1)
                sigmoid(1, k - 1)
        transpose_vh(1)
        copy_vh(1)
        quantise(1)
        for n in range(X_BUFS, X_BUFS + 3):
            load_x(n)
        load_seq(2)

        for g in range(2):
            regroup_pool(2, g, R_POOL[g])
            regroup_act(2, g, R_POOL[g], H)
        for j in range(2):
            mul_2(0, j)
            project(0, j)
        mix(3, 0)
        transpose_x(4, 0)
        scale_x(4, 0)
        mix(3, 1)
        transpose_x(4, 1)
        scale_x(4, 1)
        gate(2, 0)
        sigmoid(2, 0)
        mix(3, 2)
        transpose_x(4, 2)
        scale_x(4, 2)
        own_2(0, 0)
        project(1, 0)
        own_2(0, 1)
        project(1, 1)
        mix(3, 3)
        transpose_x(4, 3)
        scale_x(4, 3)
        gate(2, 1)
        sigmoid(2, 1)
        for j in range(2):
            gate(3, j)
        quantise(2)
        for j in range(2):
            sub_2(0, j)
        store(0)
        for j in range(2):
            sub_1(1, j)
        load_x(X_BUFS + 3)
        load_seq(3)

        for n in range(4, N_STEPS - 1):
            regroup_pool(n - 1, 0, R_POOL[0])
            regroup_act(n - 1, 0, R_POOL[0], H)
            mul_1(n - 3, 0)
            mul_1(n - 3, 1)
            mix(n, 0)
            transpose_x(n + 1, 0)
            sigmoid(n - 1, 0)
            regroup_act(n - 1, 1, R_POOL[1], H)
            regroup_pool(n - 1, 1, R_POOL[1])
            mix(n, 1)
            transpose_x(n + 1, 1)
            sigmoid(n - 1, 1)
            scale_x(n + 1, 0)
            add_1(n - 3, 0)
            project(n - 2, 0)
            if n % 2 == 0:
                transpose_vh(n // 2)
            mix(n, 2)
            transpose_x(n + 1, 2)
            scale_x(n + 1, 1)
            add_1(n - 3, 1)
            store(n - 3)
            project(n - 2, 1)
            scale_x(n + 1, 2)
            if n % 2 == 0:
                copy_vh(n // 2)
            mix(n, 3)
            transpose_x(n + 1, 3)
            scale_x(n + 1, 3)
            gate(n, 0)
            gate(n, 1)
            quantise(n - 1)
            sub_1(n - 2, 0)
            sub_1(n - 2, 1)
            if n + X_BUFS < N_STEPS:
                load_x(n + X_BUFS)
            if n % 2 == 1 and n // 2 + 2 < B:
                load_seq(n // 2 + 2)

        n = N_STEPS - 1
        regroup_pool(n - 1, 0, R_POOL[0])
        regroup_act(n - 1, 0, R_POOL[0], H)
        for j in range(2):
            mul_1(n - 3, j)
        mix(n, 0)
        gate(n, 0, "xt", 4)
        for j in range(2):
            sigmoid(n - 1, j)
        regroup_act(n - 1, 1, 0, H)
        mix(n, 1)
        gate(n, 1, "xt", 4)
        regroup_act(n, 0, 0, H)
        mix(n, 2)
        mix(n, 3)
        for j in range(2):
            mul_2(n - 2, j)
        for j in range(2):
            add_1(n - 3, j)
            project(n - 2, j)
        store(n - 3)
        mul_2(n - 1, 0)
        quantise(n - 1)
        for j in range(2):
            project(n - 1, j, "xt", 4)
        mul_2(n - 1, 1)
        regroup_act(n, 1, 0, H)
        for j in range(2):
            sigmoid(n, j)
        for j in range(2):
            own_2(n - 2, j)
        quantise(n, (0, 1))
        quantise(n, (1, 2))
        for j in range(2):
            project(n, j, "xt", 4)
        for j in range(2):
            sub_2(n - 2, j)
        store(n - 2)
        for j in range(2):
            own_2(n - 1, j)
        for j in range(2):
            sub_2(n - 1, j, nc.vector)
        store(n - 1)
        for j in range(2):
            mul_2(n, j)
        for j in range(2):
            own_2(n, j)
        for j in range(2):
            sub_2(n, j, nc.vector)
            store_half(n, j)
